import numpy as np
import ml_dtypes


def mxq(x, axis, fmt="e4m3"):
    dtype, down = {"e4m3": (ml_dtypes.float8_e4m3fn, 7), "e5m2": (ml_dtypes.float8_e5m2, 14)}[fmt]
    v = np.moveaxis(np.asarray(x, np.float32).astype(ml_dtypes.bfloat16).astype(np.float64), axis, -1)
    blocks = v.reshape(v.shape[:-1] + (-1, 32))
    amax = np.abs(blocks).max(-1, keepdims=True)
    byte = np.maximum(np.where(amax > 0, np.frexp(amax)[1] - 1 + 127, 0) - down, 1)
    scale = np.exp2(byte - 127.0)
    codes = (blocks / scale).astype(np.float32).astype(dtype).astype(np.float64)
    return np.moveaxis((codes * scale).reshape(v.shape), -1, axis)


WIDE = False


def mx_kscale(k):
    if not WIDE:
        return np.ones(k)
    levels = np.array([10, -10, 5, -5, 0])
    a = np.random.permutation(np.resize(levels, k // 512 * 4)).reshape(k // 512, 4)
    idx = np.arange(k)
    return np.exp2(a[idx // 512, idx % 128 // 32])


BF16 = ml_dtypes.bfloat16


def bf(x):
    return np.asarray(x, np.float32).astype(BF16)


def f64(x):
    return np.asarray(x).astype(np.float64)


B, N = 2048, 1024
EPS = 1e-5
DECAY = 0.9
SLOPE = 0.01


def layer_norm(v, g, b):
    mu = v.mean(-1, keepdims=True)
    var = ((v - mu) ** 2).mean(-1, keepdims=True)
    return (v - mu) / np.sqrt(var + EPS) * g + b


def sigmoid(v):
    return 1.0 / (1.0 + np.exp(-v))


def setup_inputs():
    s = mx_kscale(N)
    rest = np.random.standard_normal(N) * 2.8 - 1.7
    return {"inputs": bf(np.random.standard_normal((B, N)) * (0.5 + np.random.random((B, 1))) + 0.3 * np.random.standard_normal((B, 1))),
            "prev_potential": bf(np.random.standard_normal((B, N)) + rest),
            "syn_weights": bf(np.random.standard_normal((N, N)) * 2.0 / np.sqrt(N) / s[:, None]),
            "gate_W": bf(np.random.standard_normal((N, N)) / np.sqrt(N)),
            "gate_b": bf(np.random.standard_normal(N) * 0.3),
            "pre_gamma": bf((1.0 + 0.1 * np.random.standard_normal(N)) * s),
            "pre_beta": bf(0.1 * np.random.standard_normal(N) * s),
            "ln_gamma": bf(1.0 + 0.1 * np.random.standard_normal(N)),
            "ln_beta": bf(0.1 * np.random.standard_normal(N))}


def reference(inputs, prev_potential, syn_weights, gate_W, gate_b, pre_gamma, pre_beta, ln_gamma, ln_beta):
    x = f64(inputs)
    x_norm = layer_norm(x, f64(pre_gamma), f64(pre_beta))
    pre = mxq(x_norm, 1, "e4m3") @ mxq(f64(syn_weights), 0, "e4m3")
    potential = DECAY * f64(prev_potential) + pre
    activation = np.where(potential >= 0, potential, SLOPE * potential)
    gate = sigmoid((mxq(x, 1, "e4m3") @ mxq(f64(gate_W), 1, "e4m3").T) + f64(gate_b))
    residual = gate * activation + (1.0 - gate) * x
    output = layer_norm(residual, f64(ln_gamma), f64(ln_beta))
    return (output, potential)

@@ -1,0 +1,507 @@
+from contextlib import ExitStack
+
+import concourse.mybir as mybir
+from concourse.masks import make_identity
+
+F32 = mybir.dt.float32
+BF16 = mybir.dt.bfloat16
+U32 = mybir.dt.uint32
+U8 = mybir.dt.uint8
+FP8X4 = mybir.dt.float8_e4m3fn_x4
+ALU = mybir.AluOpType
+ACT = mybir.ActivationFunctionType
+
+P = 128
+B = 2048
+N = 1024
+NT = 16
+NQ = 8
+EPS = 1e-5
+DECAY = 0.9
+SLOPE = 0.01
+FLOPS = 2 * 2 * B * N * N
+
+MANUAL = False
+RG_ON_S = False
+GW_EXIT_ON_S = False
+
+
+def tile_mnelayer_pa_kernel(
+    tc, inputs, prev_potential, syn_weights, gate_W, gate_b, pre_gamma, pre_beta, ln_gamma, ln_beta, out_0, out_1
+):
+    nc = tc.nc
+    x_v = inputs.rearrange("(p i) k -> p i k", i=NT)
+    pv_v = prev_potential.rearrange("(p i) k -> p i k", i=NT)
+    o0_v = out_0.rearrange("(p i) n -> p i n", i=NT)
+    o1_v = out_1.rearrange("(p i) n -> p i n", i=NT)
+    syn_v = syn_weights.rearrange("(c t p) n -> c p t n", t=4, p=P)
+    gw_v = gate_W.rearrange("(h j m) k -> h m j k", j=4, m=P)
+
+    with ExitStack() as ctx:
+        if MANUAL:
+            ctx.enter_context(tc.manual_schedule())
+        res = ctx.enter_context(tc.tile_pool(name="res", bufs=1))
+        pro = ctx.enter_context(tc.tile_pool(name="pro", bufs=2))
+        sml = ctx.enter_context(tc.tile_pool(name="sml", bufs=4))
+        ps = ctx.enter_context(tc.psum_pool(name="ps", bufs=2))
+
+        idf = res.tile([P, P], F32, name="idf")
+        make_identity(nc, idf[:])
+        idb = res.tile([P, P], BF16, name="idb")
+        make_identity(nc, idb[:])
+        mh = res.tile([P, 2], F32, name="mh")
+        nc.gpsimd.memset(mh[:], -0.5)
+        vec = res.tile([P, P], BF16, name="vec")
+        nc.vector.memset(vec[:], 0.0)
+        d0 = res.tile([P, 1], F32, name="d0")
+        nc.vector.memset(d0[:], 0.0)
+        d1 = res.tile([P, 1], F32, name="d1")
+        nc.scalar.activation(out=d1[:], in_=d0[:], func=ACT.Sigmoid)
+
+        x_t = [res.tile([P, 2 * N], BF16, name="x%d" % q) for q in range(NQ)]
+        pv_t = [res.tile([P, 2 * N], BF16, name="pv%d" % q) for q in range(NQ)]
+        g_b = res.tile([P, N], BF16, name="g_b")
+        b_b = res.tile([P, N], BF16, name="b_b")
+
+        def load_x(q):
+            nc.sync.dma_start(out=x_t[q][:].rearrange("p (i k) -> p i k", i=2), in_=x_v[:, 2 * q : 2 * q + 2, :])
+
+        def load_pv(q):
+            nc.sync.dma_start(out=pv_t[q][:].rearrange("p (i k) -> p i k", i=2), in_=pv_v[:, 2 * q : 2 * q + 2, :])
+
+        sc = res.tile([P, 2 * N], U32, name="sc", align_bytes=64)
+        ss = res.tile([P, 2 * N], U8, name="ss", align_bytes=64)
+        gwc = res.tile([P, 2 * N], U32, name="gwc", align_bytes=64)
+        gws = res.tile([P, 2 * N], U8, name="gws", align_bytes=64)
+        vT = res.tile([P, 32], F32, name="vT")
+
+        st = {}
+
+        def xT_pe(q):
+            xw = x_t[q][:].bitcast(F32)
+            banks = []
+            for g in range(2):
+                bank = ps.tile([P, 512], F32, tag="tin", name="xbank")
+                for u in range(2):
+                    b = 2 * g + u
+                    for ii in range(2):
+                        nc.tensor.transpose(
+                            out=bank[:, 256 * u + 128 * ii : 256 * u + 128 * ii + 128],
+                            in_=xw[:, 512 * ii + 128 * b : 512 * ii + 128 * b + 128],
+                            identity=idf[:],
+                        )
+                banks.append(bank)
+            st["xbank"] = banks
+
+        def xT_exit(q):
+            tiles = []
+            for g in range(2):
+                xg = pro.tile([P, 1024], BF16, tag="xg", name="xg", align_bytes=64)
+                nc.scalar.copy(
+                    out=xg[:].bitcast(F32).rearrange("p (r u) -> p r u", u=2),
+                    in_=st["xbank"][g][:].rearrange("p (u r) -> p r u", u=2),
+                )
+                tiles.append(xg)
+            st["xg"] = tiles
+
+        def q_x(q):
+            xc = pro.tile([P, 512], U32, tag="xc", name="xc", align_bytes=64)
+            xs = pro.tile([P, 512], U8, tag="xs", name="xs", align_bytes=64)
+            for g in range(2):
+                nc.vector.quantize_mx(
+                    out=xc[:, 256 * g : 256 * g + 256].bitcast(FP8X4),
+                    scales=xs[:, 256 * g : 256 * g + 256],
+                    in_=st["xg"][g][:],
+                )
+            st["xc"] = xc
+            st["xs"] = xs
+
+        def stats_a(q):
+            sx = sml.tile([P, 2], F32, tag="sx", name="sx")
+            for ii in range(2):
+                junk = pro.tile([P, N], BF16, tag="junk", name="junk")
+                nc.scalar.activation(
+                    out=junk[:], in_=x_t[q][:, N * ii : N * ii + N], func=ACT.Identity, accum_out=sx[:, ii : ii + 1]
+                )
+            nm = sml.tile([P, 2], F32, tag="nm", name="nm")
+            nc.scalar.mul(out=nm[:], in_=sx[:], mul=-1.0 / N)
+            st["nm"] = nm
+
+        def stats_b(q):
+            nm = st["nm"]
+            sq = sml.tile([P, 2], F32, tag="sq", name="sq")
+            for ii in range(2):
+                junk = pro.tile([P, N], BF16, tag="junk", name="junk")
+                nc.scalar.activation(
+                    out=junk[:],
+                    in_=x_t[q][:, N * ii : N * ii + N],
+                    func=ACT.Square,
+                    bias=nm[:, ii : ii + 1],
+                    accum_out=sq[:, ii : ii + 1],
+                )
+            va = sml.tile([P, 2], F32, tag="va", name="va")
+            nc.gpsimd.tensor_scalar(out=va[:], in0=sq[:], scalar1=1.0 / N, scalar2=EPS, op0=ALU.mult, op1=ALU.add)
+            rs = sml.tile([P, 2], F32, tag="rs", name="rs")
+            nc.gpsimd.tensor_tensor(out=rs[:], in0=va[:], in1=mh[:], op=ALU.pow)
+            nr = sml.tile([P, 2], F32, tag="nr", name="nr")
+            nc.gpsimd.tensor_tensor(out=nr[:], in0=nm[:], in1=rs[:], op=ALU.mult)
+            st["rs"] = rs
+            st["nr"] = nr
+
+        def z_c(q):
+            z = pro.tile([P, 2 * N], F32, tag="z", name="z")
+            for ii in range(2):
+                nc.scalar.activation(
+                    out=z[:, N * ii : N * ii + N],
+                    in_=x_t[q][:, N * ii : N * ii + N],
+                    func=ACT.Identity,
+                    scale=st["rs"][:, ii : ii + 1],
+                    bias=st["nr"][:, ii : ii + 1],
+                )
+            st["z"] = z
+
+        def regroup(c, on_s):
+            zg = pro.tile([P, 1024], BF16, tag="zg", name="zg", align_bytes=64)
+            src = st["zp"][c][:].rearrange("p (t a i) -> p a t i", t=4, i=4)
+            dst = zg[:].rearrange("p (a i t) -> p a t i", i=4, t=4)
+            if on_s:
+                nc.scalar.copy(out=dst, in_=src)
+            else:
+                nc.vector.tensor_copy(out=dst, in_=src)
+            st["zg"][c] = zg
+
+        def zT_e(q):
+            z = st["z"]
+            st["zp"] = [None, None]
+            st["zg"] = [None, None]
+            for c in range(2):
+                zp = pro.tile([P, 1024], BF16, tag="zp", name="zp")
+                for jh in range(2):
+                    bank = ps.tile([P, 512], F32, tag="tin", name="zbank")
+                    for jj in range(2):
+                        j = 4 * c + 2 * jh + jj
+                        for ii in range(2):
+                            nc.tensor.transpose(
+                                out=bank[:, 256 * jj + 128 * ii : 256 * jj + 128 * ii + 128],
+                                in_=z[:, N * ii + 128 * j : N * ii + 128 * j + 128],
+                                identity=idf[:],
+                            )
+                    for jj in range(2):
+                        j = 4 * c + 2 * jh + jj
+                        t = 2 * jh + jj
+                        nc.scalar.activation(
+                            out=zp[:, 256 * t : 256 * t + 256],
+                            in_=bank[:, 256 * jj : 256 * jj + 256],
+                            func=ACT.Identity,
+                            scale=vT[:, 8 + j : 9 + j],
+                            bias=vT[:, 16 + j : 17 + j],
+                        )
+                st["zp"][c] = zp
+                if RG_ON_S:
+                    regroup(c, True)
+            zc = pro.tile([P, 512], U32, tag="zc", name="zc", align_bytes=64)
+            zs = pro.tile([P, 512], U8, tag="zs", name="zs", align_bytes=64)
+            st["zc_next"] = zc
+            st["zs_next"] = zs
+
+        def rg_v(c):
+            if not RG_ON_S:
+                regroup(c, False)
+
+        def q_z(c):
+            nc.vector.quantize_mx(
+                out=st["zc_next"][:, 256 * c : 256 * c + 256].bitcast(FP8X4),
+                scales=st["zs_next"][:, 256 * c : 256 * c + 256],
+                in_=st["zg"][c][:],
+            )
+
+        load_x(0)
+        nc.sync.dma_start(out=vec[0:8, :], in_=gate_b.rearrange("(j m) -> j m", m=P))
+        nc.sync.dma_start(out=vec[8:16, :], in_=pre_gamma.rearrange("(j m) -> j m", m=P))
+        nc.sync.dma_start(out=vec[16:24, :], in_=pre_beta.rearrange("(j m) -> j m", m=P))
+        with tc.tile_pool(name="wt", bufs=1) as wt:
+            sraw = []
+            for c in range(2):
+                raw = wt.tile([P, 4 * N], BF16, tag="wraw", name="sraw", bufs=4)
+                nc.sync.dma_start(out=raw[:].rearrange("p (t n) -> p t n", t=4), in_=syn_v[c])
+                sraw.append(raw)
+            graw = []
+            for h in range(2):
+                raw = wt.tile([P, 4 * N], BF16, tag="wraw", name="graw", bufs=4)
+                nc.sync.dma_start(out=raw[:].rearrange("p (j k) -> p j k", j=4), in_=gw_v[h])
+                graw.append(raw)
+            load_x(1)
+            load_pv(0)
+            nc.sync.dma_start(out=g_b[:], in_=ln_gamma.partition_broadcast(P))
+            nc.sync.dma_start(out=b_b[:], in_=ln_beta.partition_broadcast(P))
+            for q in range(2, NQ):
+                load_x(q)
+                load_pv(q - 1)
+            load_pv(NQ - 1)
+
+            vbank = ps.tile([P, P], BF16, tag="tin", name="vbank")
+            nc.tensor.transpose(out=vbank[:], in_=vec[:], identity=idb[:])
+            nc.vector.tensor_copy(out=vT[:, 0:24], in_=vbank[:, 0:24])
+
+            xT_pe(0)
+            xT_exit(0)
+            stats_a(0)
+            stats_b(0)
+
+            def syn_prep(c):
+                grps = []
+                for h in range(2):
+                    grp = wt.tile([P, 2048], BF16, tag="wgrp", name="sgrp", bufs=3, align_bytes=64)
+                    nc.vector.tensor_copy(
+                        out=grp[:].rearrange("p (a i t) -> p a t i", i=4, t=4),
+                        in_=sraw[c][:].rearrange("p (t n) -> p t n", t=4)[:, :, 512 * h : 512 * h + 512].rearrange(
+                            "p t (a i) -> p a t i", i=4
+                        ),
+                    )
+                    grps.append(grp)
+                for h in range(2):
+                    o = N * c + 512 * h
+                    nc.vector.quantize_mx(
+                        out=sc[:, o : o + 512].bitcast(FP8X4), scales=ss[:, o : o + 512], in_=grps[h][:]
+                    )
+
+            syn_prep(0)
+            q_x(0)
+            z_c(0)
+            syn_prep(1)
+            zT_e(0)
+
+            def gw_prep(h):
+                gww = graw[h][:].bitcast(F32)
+                grps = []
+                for g in range(2):
+                    grp = wt.tile([P, 2048], BF16, tag="wgrp", name="ggrp", bufs=3, align_bytes=64)
+                    grw = grp[:].bitcast(F32)
+                    for jq in range(2):
+                        bank = ps.tile([P, 512], F32, tag="tin", name="gbank")
+                        for u in range(2):
+                            b = 2 * g + u
+                            for j2 in range(2):
+                                j = 2 * jq + j2
+                                nc.tensor.transpose(
+                                    out=bank[:, 256 * u + 128 * j2 : 256 * u + 128 * j2 + 128],
+                                    in_=gww[:, 512 * j + 128 * b : 512 * j + 128 * b + 128],
+                                    identity=idf[:],
+                                )
+                        dst = grw[:, 512 * jq : 512 * jq + 512].rearrange("p (n u) -> p n u", u=2)
+                        src = bank[:].rearrange("p (u n) -> p n u", u=2)
+                        if GW_EXIT_ON_S:
+                            nc.scalar.copy(out=dst, in_=src)
+                        else:
+                            nc.vector.tensor_copy(out=dst, in_=src)
+                    grps.append(grp)
+                for g in range(2):
+                    o = N * g + 512 * h
+                    nc.vector.quantize_mx(
+                        out=gwc[:, o : o + 512].bitcast(FP8X4), scales=gws[:, o : o + 512], in_=grps[g][:]
+                    )
+
+            gw_prep(0)
+            rg_v(0)
+            rg_v(1)
+            q_z(0)
+            q_z(1)
+            gw_prep(1)
+
+        epi = ctx.enter_context(tc.tile_pool(name="epi", bufs=3))
+
+        def gate(q):
+            gts = epi.tile([P, 2048], F32, tag="gts", name="gts", bufs=2)
+            xc = st["xc"]
+            xs = st["xs"]
+            for jp in range(4):
+                bank = ps.tile([P, 512], F32, tag="gt", name="gtbank")
+                for jj in range(2):
+                    j = 2 * jp + jj
+                    for g in range(2):
+                        o = N * g + 128 * j
+                        nc.tensor.matmul_mx(
+                            out=bank[:, 256 * jj : 256 * jj + 256],
+                            lhsT=gwc[:, o : o + 128].bitcast(FP8X4),
+                            lhsT_scale=gws[:, o : o + 128],
+                            rhs=xc[:, 256 * g : 256 * g + 256].bitcast(FP8X4),
+                            rhs_scale=xs[:, 256 * g : 256 * g + 256],
+                            start=(g == 0),
+                            stop=(g == 1),
+                        )
+                for jj in range(2):
+                    j = 2 * jp + jj
+                    nc.scalar.activation(
+                        out=gts[:, 256 * j : 256 * j + 256],
+                        in_=bank[:, 256 * jj : 256 * jj + 256],
+                        func=ACT.Sigmoid,
+                        bias=vT[:, j : j + 1],
+                    )
+            st["gts_next"] = gts
+
+        ep = {}
+
+        def gback(t, gts):
+            ii = t % 2
+            banks = []
+            for h in range(2):
+                bank = ps.tile([P, 512], F32, tag="gb", name="gbbank")
+                for jj in range(4):
+                    j = 4 * h + jj
+                    nc.tensor.transpose(
+                        out=bank[:, 128 * jj : 128 * jj + 128],
+                        in_=gts[:, 256 * j + 128 * ii : 256 * j + 128 * ii + 128],
+                        identity=idf[:],
+                    )
+                banks.append(bank)
+            ep[("gb", t)] = banks
+
+        def syn_mx(t, zc, zs):
+            ii = t % 2
+            banks = []
+            for h in range(2):
+                bank = ps.tile([P, 512], F32, tag="pre", name="prebank")
+                for c in range(2):
+                    o = 256 * c + 128 * ii
+                    w = N * c + 512 * h
+                    nc.tensor.matmul_mx(
+                        out=bank[:],
+                        lhsT=zc[:, o : o + 128].bitcast(FP8X4),
+                        lhsT_scale=zs[:, o : o + 128],
+                        rhs=sc[:, w : w + 512].bitcast(FP8X4),
+                        rhs_scale=ss[:, w : w + 512],
+                        start=(c == 0),
+                        stop=(c == 1),
+                    )
+                banks.append(bank)
+            ep[("pre", t)] = banks
+
+        def xs_of(t):
+            return x_t[t // 2][:, N * (t % 2) : N * (t % 2) + N]
+
+        def op_g(t):
+            pt = epi.tile([P, N], F32, tag="p", name="pt")
+            pv = pv_t[t // 2]
+            o = N * (t % 2)
+            for h in range(2):
+                nc.vector.scalar_tensor_tensor(
+                    out=pt[:, 512 * h : 512 * h + 512],
+                    in0=pv[:, o + 512 * h : o + 512 * h + 512],
+                    scalar=DECAY,
+                    in1=ep[("pre", t)][h][:],
+                    op0=ALU.mult,
+                    op1=ALU.add,
+                )
+            nc.sync.dma_start(out=o1_v[:, t, :], in_=pt[:])
+            ep[("p", t)] = pt
+
+        def op_i(t):
+            w = epi.tile([P, N], F32, tag="w", name="w", bufs=4)
+            pt = ep[("p", t)]
+            nc.vector.scalar_tensor_tensor(out=w[:], in0=pt[:], scalar=SLOPE, in1=pt[:], op0=ALU.mult, op1=ALU.max)
+            ep[("w", t)] = w
+
+        def op_j(t):
+            w = ep[("w", t)]
+            nc.vector.tensor_tensor(out=w[:], in0=w[:], in1=xs_of(t), op=ALU.subtract)
+
+        def op_k(t):
+            w = ep[("w", t)]
+            for h in range(2):
+                nc.vector.tensor_tensor(
+                    out=w[:, 512 * h : 512 * h + 512],
+                    in0=w[:, 512 * h : 512 * h + 512],
+                    in1=ep[("gb", t)][h][:],
+                    op=ALU.mult,
+                )
+
+        def op_l(t):
+            w = ep[("w", t)]
+            sr = sml.tile([P, 1], F32, tag="sr", name="sr")
+            nc.vector.scalar_tensor_tensor(
+                out=w[:], in0=w[:], scalar=1.0, in1=xs_of(t), op0=ALU.mult, op1=ALU.add, accum_out=sr[:]
+            )
+            nm2 = sml.tile([P, 1], F32, tag="nm2", name="nm2")
+            nc.vector.tensor_scalar(out=nm2[:], in0=sr[:], scalar1=-1.0 / N, scalar2=None, op0=ALU.mult)
+            ep[("nm2", t)] = nm2
+
+        def op_m(t):
+            w = ep[("w", t)]
+            sq2 = sml.tile([P, 1], F32, tag="sq2", name="sq2")
+            junk = pro.tile([P, N], BF16, tag="junk", name="junk")
+            nc.scalar.activation(out=junk[:], in_=w[:], func=ACT.Square, bias=ep[("nm2", t)][:], accum_out=sq2[:])
+            v2 = sml.tile([P, 1], F32, tag="v2", name="v2")
+            nc.gpsimd.tensor_scalar(out=v2[:], in0=sq2[:], scalar1=1.0 / N, scalar2=EPS, op0=ALU.mult, op1=ALU.add)
+            rs2 = sml.tile([P, 1], F32, tag="rs2", name="rs2")
+            nc.gpsimd.tensor_tensor(out=rs2[:], in0=v2[:], in1=mh[:, 0:1], op=ALU.pow)
+            ep[("rs2", t)] = rs2
+
+        def op_n(t):
+            o = epi.tile([P, N], F32, tag="o", name="o")
+            nc.vector.scalar_tensor_tensor(
+                out=o[:], in0=ep[("w", t)][:], scalar=ep[("nm2", t)][:], in1=g_b[:], op0=ALU.add, op1=ALU.mult
+            )
+            ep[("o", t)] = o
+
+        def op_o(t):
+            o = ep[("o", t)]
+            nc.vector.scalar_tensor_tensor(
+                out=o[:], in0=o[:], scalar=ep[("rs2", t)][:], in1=b_b[:], op0=ALU.mult, op1=ALU.add
+            )
+            nc.sync.dma_start(out=o0_v[:, t, :], in_=o[:])
+
+        gate(0)
+        cur = {"gts": st["gts_next"], "zc": st["zc_next"], "zs": st["zs_next"]}
+        gback(0, cur["gts"])
+        xT_pe(1)
+        syn_mx(0, cur["zc"], cur["zs"])
+
+        for q in range(NQ):
+            nx = q + 1 < NQ
+            t0 = 2 * q
+            t1 = 2 * q + 1
+            if nx:
+                xT_exit(q + 1)
+            op_g(t0)
+            syn_mx(t1, cur["zc"], cur["zs"])
+            if nx:
+                stats_a(q + 1)
+            op_i(t0)
+            op_j(t0)
+            op_k(t0)
+            gback(t1, cur["gts"])
+            if nx:
+                stats_b(q + 1)
+            op_l(t0)
+            if nx:
+                q_x(q + 1)
+            op_m(t0)
+            if nx:
+                z_c(q + 1)
+            op_g(t1)
+            op_i(t1)
+            op_j(t1)
+            op_k(t1)
+            op_l(t1)
+            if nx:
+                gate(q + 1)
+            op_m(t1)
+            if nx:
+                zT_e(q + 1)
+            op_n(t0)
+            if nx:
+                rg_v(0)
+            op_o(t0)
+            if nx:
+                q_z(0)
+                rg_v(1)
+            op_n(t1)
+            if nx:
+                q_z(1)
+            op_o(t1)
+            if nx:
+                cur = {"gts": st["gts_next"], "zc": st["zc_next"], "zs": st["zs_next"]}
+                gback(t0 + 2, cur["gts"])
+                if q + 2 < NQ:
+                    xT_pe(q + 2)
+                syn_mx(t0 + 2, cur["zc"], cur["zs"])

@@ -21,9 +21,9 @@ DECAY = 0.9
 SLOPE = 0.01
 FLOPS = 2 * 2 * B * N * N
 
-MANUAL = False
-RG_ON_S = False
-GW_EXIT_ON_S = False
+MANUAL = True
+RG_ON_S = True
+NP_SPLIT = 0
 
 
 def tile_mnelayer_pa_kernel(
@@ -55,6 +55,10 @@ def tile_mnelayer_pa_kernel(
         nc.vector.memset(vec[:], 0.0)
         d0 = res.tile([P, 1], F32, name="d0")
         nc.vector.memset(d0[:], 0.0)
+        ones = res.tile([P, 32], BF16, name="ones")
+        nc.vector.memset(ones[:], 1.0)
+        eps_t = res.tile([P, 1], F32, name="eps_t")
+        nc.vector.memset(eps_t[:], EPS)
         d1 = res.tile([P, 1], F32, name="d1")
         nc.scalar.activation(out=d1[:], in_=d0[:], func=ACT.Sigmoid)
 
@@ -62,6 +66,11 @@ def tile_mnelayer_pa_kernel(
         pv_t = [res.tile([P, 2 * N], BF16, name="pv%d" % q) for q in range(NQ)]
         g_b = res.tile([P, N], BF16, name="g_b")
         b_b = res.tile([P, N], BF16, name="b_b")
+        sc = res.tile([P, 2 * N], U32, name="sc", align_bytes=64)
+        ss = res.tile([P, 2 * N], U8, name="ss", align_bytes=64)
+        gwc = res.tile([P, 2 * N], U32, name="gwc", align_bytes=64)
+        gws = res.tile([P, 2 * N], U8, name="gws", align_bytes=64)
+        vT = res.tile([P, 32], F32, name="vT")
 
         def load_x(q):
             nc.sync.dma_start(out=x_t[q][:].rearrange("p (i k) -> p i k", i=2), in_=x_v[:, 2 * q : 2 * q + 2, :])
@@ -69,16 +78,22 @@ def tile_mnelayer_pa_kernel(
         def load_pv(q):
             nc.sync.dma_start(out=pv_t[q][:].rearrange("p (i k) -> p i k", i=2), in_=pv_v[:, 2 * q : 2 * q + 2, :])
 
-        sc = res.tile([P, 2 * N], U32, name="sc", align_bytes=64)
-        ss = res.tile([P, 2 * N], U8, name="ss", align_bytes=64)
-        gwc = res.tile([P, 2 * N], U32, name="gwc", align_bytes=64)
-        gws = res.tile([P, 2 * N], U8, name="gws", align_bytes=64)
-        vT = res.tile([P, 32], F32, name="vT")
-
         st = {}
+        epi_box = []
 
-        def xT_pe(q):
-            xw = x_t[q][:].bitcast(F32)
+        def okr(r):
+            return 0 <= r < NQ
+
+        def okt(t):
+            return 0 <= t < NT
+
+        def x_of(t):
+            return x_t[t // 2][:, N * (t % 2) : N * (t % 2) + N]
+
+        def xT_pe(r):
+            if not okr(r):
+                return
+            xw = x_t[r][:].bitcast(F32)
             banks = []
             for g in range(2):
                 bank = ps.tile([P, 512], F32, tag="tin", name="xbank")
@@ -91,131 +106,374 @@ def tile_mnelayer_pa_kernel(
                             identity=idf[:],
                         )
                 banks.append(bank)
-            st["xbank"] = banks
+            st[("xbank", r)] = banks
 
-        def xT_exit(q):
+        def dd(r):
+            if not okr(r):
+                return
             tiles = []
             for g in range(2):
-                xg = pro.tile([P, 1024], BF16, tag="xg", name="xg", align_bytes=64)
+                xg = pro.tile([P, 1024], BF16, tag="xg", name="xg", align_bytes=64, bufs=4)
                 nc.scalar.copy(
                     out=xg[:].bitcast(F32).rearrange("p (r u) -> p r u", u=2),
-                    in_=st["xbank"][g][:].rearrange("p (u r) -> p r u", u=2),
+                    in_=st[("xbank", r)][g][:].rearrange("p (u r) -> p r u", u=2),
                 )
                 tiles.append(xg)
-            st["xg"] = tiles
+            st[("xg", r)] = tiles
 
-        def q_x(q):
+        def qx(r):
+            if not okr(r):
+                return
             xc = pro.tile([P, 512], U32, tag="xc", name="xc", align_bytes=64)
             xs = pro.tile([P, 512], U8, tag="xs", name="xs", align_bytes=64)
             for g in range(2):
                 nc.vector.quantize_mx(
                     out=xc[:, 256 * g : 256 * g + 256].bitcast(FP8X4),
                     scales=xs[:, 256 * g : 256 * g + 256],
-                    in_=st["xg"][g][:],
+                    in_=st[("xg", r)][g][:],
                 )
-            st["xc"] = xc
-            st["xs"] = xs
+            st[("xc", r)] = (xc, xs)
 
-        def stats_a(q):
-            sx = sml.tile([P, 2], F32, tag="sx", name="sx")
+        def pe_sum(r):
+            if not okr(r):
+                return
+            bank = ps.tile([P, 64], F32, tag="tin", name="sbank")
             for ii in range(2):
-                junk = pro.tile([P, N], BF16, tag="junk", name="junk")
-                nc.scalar.activation(
-                    out=junk[:], in_=x_t[q][:, N * ii : N * ii + N], func=ACT.Identity, accum_out=sx[:, ii : ii + 1]
-                )
-            nm = sml.tile([P, 2], F32, tag="nm", name="nm")
-            nc.scalar.mul(out=nm[:], in_=sx[:], mul=-1.0 / N)
-            st["nm"] = nm
+                for g in range(2):
+                    xv = st[("xg", r)][g][:].rearrange("p (r t) -> p r t", t=4)
+                    for t in range(4):
+                        nc.tensor.matmul(
+                            out=bank[:, 32 * ii : 32 * ii + 32],
+                            lhsT=xv[:, 128 * ii : 128 * ii + 128, t],
+                            rhs=ones[:],
+                            start=(g == 0 and t == 0),
+                            stop=(g == 1 and t == 3),
+                        )
+            st[("sbank", r)] = bank
 
-        def stats_b(q):
-            nm = st["nm"]
+        def nm_s(r):
+            if not okr(r):
+                return
+            nm = sml.tile([P, 2], F32, tag="nm", name="nm", bufs=6)
+            nc.scalar.mul(
+                out=nm[:], in_=st[("sbank", r)][:].rearrange("p (i c) -> p i c", c=32)[:, :, 0], mul=-1.0 / N
+            )
+            st[("nm", r)] = nm
+
+        def bb(r):
+            if not okr(r):
+                return
+            nm = st[("nm", r)]
             sq = sml.tile([P, 2], F32, tag="sq", name="sq")
             for ii in range(2):
                 junk = pro.tile([P, N], BF16, tag="junk", name="junk")
                 nc.scalar.activation(
                     out=junk[:],
-                    in_=x_t[q][:, N * ii : N * ii + N],
+                    in_=x_t[r][:, N * ii : N * ii + N],
                     func=ACT.Square,
                     bias=nm[:, ii : ii + 1],
                     accum_out=sq[:, ii : ii + 1],
                 )
             va = sml.tile([P, 2], F32, tag="va", name="va")
-            nc.gpsimd.tensor_scalar(out=va[:], in0=sq[:], scalar1=1.0 / N, scalar2=EPS, op0=ALU.mult, op1=ALU.add)
+            nc.scalar.activation(out=va[:], in_=sq[:], func=ACT.Identity, scale=1.0 / N, bias=eps_t[:])
+            st[("va", r)] = va
+
+        def powx(r):
+            if not okr(r):
+                return
             rs = sml.tile([P, 2], F32, tag="rs", name="rs")
-            nc.gpsimd.tensor_tensor(out=rs[:], in0=va[:], in1=mh[:], op=ALU.pow)
+            nc.gpsimd.tensor_tensor(out=rs[:], in0=st[("va", r)][:], in1=mh[:], op=ALU.pow)
             nr = sml.tile([P, 2], F32, tag="nr", name="nr")
-            nc.gpsimd.tensor_tensor(out=nr[:], in0=nm[:], in1=rs[:], op=ALU.mult)
-            st["rs"] = rs
-            st["nr"] = nr
+            nc.gpsimd.tensor_tensor(out=nr[:], in0=st[("nm", r)][:], in1=rs[:], op=ALU.mult)
+            st[("rs", r)] = (rs, nr)
 
-        def z_c(q):
-            z = pro.tile([P, 2 * N], F32, tag="z", name="z")
-            for ii in range(2):
+        def cc(r, tv):
+            if okr(r):
+                z = pro.tile([P, 2 * N], F32, tag="z", name="z")
+                rs, nr = st[("rs", r)]
+                for ii in range(2):
+                    nc.scalar.activation(
+                        out=z[:, N * ii : N * ii + N],
+                        in_=x_t[r][:, N * ii : N * ii + N],
+                        func=ACT.Identity,
+                        scale=rs[:, ii : ii + 1],
+                        bias=nr[:, ii : ii + 1],
+                    )
+                    if ii == 0:
+                        v2(tv)
+                st[("z", r)] = z
+            else:
+                v2(tv)
+
+        def zT_bank(r, b):
+            if not okr(r):
+                return
+            z = st[("z", r)]
+            bank = ps.tile([P, 512], F32, tag="tin", name="zbank")
+            for jj in range(2):
+                j = 2 * b + jj
+                for ii in range(2):
+                    nc.tensor.transpose(
+                        out=bank[:, 256 * jj + 128 * ii : 256 * jj + 128 * ii + 128],
+                        in_=z[:, N * ii + 128 * j : N * ii + 128 * j + 128],
+                        identity=idf[:],
+                    )
+            st[("zbank", r, b)] = bank
+
+        def e_bank(r, b):
+            if not okr(r):
+                return
+            c = b // 2
+            if b % 2 == 0:
+                st[("zp", r, c)] = pro.tile([P, 1024], BF16, tag="zp", name="zp")
+            zp = st[("zp", r, c)]
+            bank = st[("zbank", r, b)]
+            for jj in range(2):
+                j = 2 * b + jj
+                t = j % 4
                 nc.scalar.activation(
-                    out=z[:, N * ii : N * ii + N],
-                    in_=x_t[q][:, N * ii : N * ii + N],
+                    out=zp[:, 256 * t : 256 * t + 256],
+                    in_=bank[:, 256 * jj : 256 * jj + 256],
                     func=ACT.Identity,
-                    scale=st["rs"][:, ii : ii + 1],
-                    bias=st["nr"][:, ii : ii + 1],
+                    scale=vT[:, 8 + j : 9 + j],
+                    bias=vT[:, 16 + j : 17 + j],
                 )
-            st["z"] = z
 
-        def regroup(c, on_s):
+        def rg(r, c, on_s):
+            if not okr(r):
+                return
             zg = pro.tile([P, 1024], BF16, tag="zg", name="zg", align_bytes=64)
-            src = st["zp"][c][:].rearrange("p (t a i) -> p a t i", t=4, i=4)
+            src = st[("zp", r, c)][:].rearrange("p (t a i) -> p a t i", t=4, i=4)
             dst = zg[:].rearrange("p (a i t) -> p a t i", i=4, t=4)
             if on_s:
                 nc.scalar.copy(out=dst, in_=src)
             else:
                 nc.vector.tensor_copy(out=dst, in_=src)
-            st["zg"][c] = zg
+            st[("zg", r, c)] = zg
 
-        def zT_e(q):
-            z = st["z"]
-            st["zp"] = [None, None]
-            st["zg"] = [None, None]
-            for c in range(2):
-                zp = pro.tile([P, 1024], BF16, tag="zp", name="zp")
-                for jh in range(2):
-                    bank = ps.tile([P, 512], F32, tag="tin", name="zbank")
-                    for jj in range(2):
-                        j = 4 * c + 2 * jh + jj
-                        for ii in range(2):
-                            nc.tensor.transpose(
-                                out=bank[:, 256 * jj + 128 * ii : 256 * jj + 128 * ii + 128],
-                                in_=z[:, N * ii + 128 * j : N * ii + 128 * j + 128],
-                                identity=idf[:],
-                            )
-                    for jj in range(2):
-                        j = 4 * c + 2 * jh + jj
-                        t = 2 * jh + jj
-                        nc.scalar.activation(
-                            out=zp[:, 256 * t : 256 * t + 256],
-                            in_=bank[:, 256 * jj : 256 * jj + 256],
-                            func=ACT.Identity,
-                            scale=vT[:, 8 + j : 9 + j],
-                            bias=vT[:, 16 + j : 17 + j],
-                        )
-                st["zp"][c] = zp
-                if RG_ON_S:
-                    regroup(c, True)
+        def qz(r):
+            if not okr(r):
+                return
             zc = pro.tile([P, 512], U32, tag="zc", name="zc", align_bytes=64)
             zs = pro.tile([P, 512], U8, tag="zs", name="zs", align_bytes=64)
-            st["zc_next"] = zc
-            st["zs_next"] = zs
+            for c in range(2):
+                nc.vector.quantize_mx(
+                    out=zc[:, 256 * c : 256 * c + 256].bitcast(FP8X4),
+                    scales=zs[:, 256 * c : 256 * c + 256],
+                    in_=st[("zg", r, c)][:],
+                )
+            st[("zc", r)] = (zc, zs)
 
-        def rg_v(c):
-            if not RG_ON_S:
-                regroup(c, False)
+        def gate_mx(r, b):
+            if not okr(r):
+                return
+            xc, xs = st[("xc", r)]
+            bank = ps.tile([P, 512], F32, tag="gt", name="gtbank")
+            for jj in range(2):
+                j = 2 * b + jj
+                for g in range(2):
+                    o = N * g + 128 * j
+                    nc.tensor.matmul_mx(
+                        out=bank[:, 256 * jj : 256 * jj + 256],
+                        lhsT=gwc[:, o : o + 128].bitcast(FP8X4),
+                        lhsT_scale=gws[:, o : o + 128],
+                        rhs=xc[:, 256 * g : 256 * g + 256].bitcast(FP8X4),
+                        rhs_scale=xs[:, 256 * g : 256 * g + 256],
+                        start=(g == 0),
+                        stop=(g == 1),
+                    )
+            st[("gtbank", r, b)] = bank
 
-        def q_z(c):
-            nc.vector.quantize_mx(
-                out=st["zc_next"][:, 256 * c : 256 * c + 256].bitcast(FP8X4),
-                scales=st["zs_next"][:, 256 * c : 256 * c + 256],
-                in_=st["zg"][c][:],
+        def h_bank(r, b):
+            if not okr(r):
+                return
+            if b == 0:
+                st[("gts", r)] = epi_box[0].tile([P, 2048], F32, tag="gts", name="gts", bufs=2)
+            gts = st[("gts", r)]
+            bank = st[("gtbank", r, b)]
+            for jj in range(2):
+                j = 2 * b + jj
+                nc.scalar.activation(
+                    out=gts[:, 256 * j : 256 * j + 256],
+                    in_=bank[:, 256 * jj : 256 * jj + 256],
+                    func=ACT.Sigmoid,
+                    bias=vT[:, j : j + 1],
+                )
+
+        def gback(t):
+            if not okt(t):
+                return
+            gts = st[("gts", t // 2)]
+            ii = t % 2
+            banks = []
+            for h in range(2):
+                bank = ps.tile([P, 512], F32, tag="gb", name="gbbank")
+                for jj in range(4):
+                    j = 4 * h + jj
+                    nc.tensor.transpose(
+                        out=bank[:, 128 * jj : 128 * jj + 128],
+                        in_=gts[:, 256 * j + 128 * ii : 256 * j + 128 * ii + 128],
+                        identity=idf[:],
+                    )
+                banks.append(bank)
+            st[("gb", t)] = banks
+
+        def syn_mx(t):
+            if not okt(t):
+                return
+            zc, zs = st[("zc", t // 2)]
+            ii = t % 2
+            banks = []
+            for h in range(2):
+                bank = ps.tile([P, 512], F32, tag="pre", name="prebank")
+                for c in range(2):
+                    o = 256 * c + 128 * ii
+                    w = N * c + 512 * h
+                    nc.tensor.matmul_mx(
+                        out=bank[:],
+                        lhsT=zc[:, o : o + 128].bitcast(FP8X4),
+                        lhsT_scale=zs[:, o : o + 128],
+                        rhs=sc[:, w : w + 512].bitcast(FP8X4),
+                        rhs_scale=ss[:, w : w + 512],
+                        start=(c == 0),
+                        stop=(c == 1),
+                    )
+                banks.append(bank)
+            st[("pre", t)] = banks
+
+        def op_g(t):
+            if not okt(t):
+                return
+            pt = epi_box[0].tile([P, N], F32, tag="p", name="pt", bufs=3)
+            pv = pv_t[t // 2]
+            o = N * (t % 2)
+            for h in range(2):
+                nc.vector.scalar_tensor_tensor(
+                    out=pt[:, 512 * h : 512 * h + 512],
+                    in0=pv[:, o + 512 * h : o + 512 * h + 512],
+                    scalar=DECAY,
+                    in1=st[("pre", t)][h][:],
+                    op0=ALU.mult,
+                    op1=ALU.add,
+                )
+            nc.sync.dma_start(out=o1_v[:, t, :], in_=pt[:])
+            st[("p", t)] = pt
+
+        def op_i(t):
+            if not okt(t):
+                return
+            w = epi_box[0].tile([P, N], F32, tag="w", name="w", bufs=4)
+            pt = st[("p", t)]
+            nc.vector.scalar_tensor_tensor(out=w[:], in0=pt[:], scalar=SLOPE, in1=pt[:], op0=ALU.mult, op1=ALU.max)
+            st[("w", t)] = w
+
+        def op_j(t):
+            if not okt(t):
+                return
+            w = st[("w", t)]
+            nc.vector.tensor_tensor(out=w[:], in0=w[:], in1=x_of(t), op=ALU.subtract)
+
+        def op_k(t):
+            if not okt(t):
+                return
+            w = st[("w", t)]
+            se = sml.tile([P, 2], F32, tag="se", name="se")
+            for h in range(2):
+                nc.vector.scalar_tensor_tensor(
+                    out=w[:, 512 * h : 512 * h + 512],
+                    in0=w[:, 512 * h : 512 * h + 512],
+                    scalar=1.0,
+                    in1=st[("gb", t)][h][:],
+                    op0=ALU.mult,
+                    op1=ALU.mult,
+                    accum_out=se[:, h : h + 1],
+                )
+            st[("se", t)] = se
+
+        def s1(t):
+            if not okt(t):
+                return
+            se = st[("se", t)]
+            s1t = sml.tile([P, 1], F32, tag="s1t", name="s1t")
+            nc.vector.tensor_tensor(out=s1t[:], in0=se[:, 0:1], in1=se[:, 1:2], op=ALU.add)
+            st[("s1t", t)] = s1t
+
+        def s2(t):
+            if not okt(t):
+                return
+            nmc = sml.tile([P, 1], F32, tag="nmc", name="nmc")
+            nc.vector.scalar_tensor_tensor(
+                out=nmc[:],
+                in0=st[("s1t", t)][:],
+                scalar=-1.0 / N,
+                in1=st[("nm", t // 2)][:, t % 2 : t % 2 + 1],
+                op0=ALU.mult,
+                op1=ALU.add,
+            )
+            st[("nmc", t)] = nmc
+
+        def op_l(t):
+            if not okt(t):
+                return
+            w = st[("w", t)]
+            nc.vector.scalar_tensor_tensor(
+                out=w[:], in0=w[:], scalar=st[("nmc", t)][:], in1=x_of(t), op0=ALU.add, op1=ALU.add
             )
 
+        def op_m(t):
+            if not okt(t):
+                return
+            sq2 = sml.tile([P, 1], F32, tag="sq2", name="sq2")
+            junk = pro.tile([P, N], BF16, tag="junk", name="junk")
+            nc.scalar.activation(out=junk[:], in_=st[("w", t)][:], func=ACT.Square, accum_out=sq2[:])
+            st[("sq2", t)] = sq2
+
+        def v2(t):
+            if not okt(t):
+                return
+            v2t = sml.tile([P, 1], F32, tag="v2t", name="v2t")
+            nc.scalar.activation(out=v2t[:], in_=st[("sq2", t)][:], func=ACT.Identity, scale=1.0 / N, bias=eps_t[:])
+            st[("v2t", t)] = v2t
+
+        def pow_r(t):
+            if not okt(t):
+                return
+            rs2 = sml.tile([P, 1], F32, tag="rs2", name="rs2")
+            nc.gpsimd.tensor_tensor(out=rs2[:], in0=st[("v2t", t)][:], in1=mh[:, 0:1], op=ALU.pow)
+            st[("rs2", t)] = rs2
+
+        def np_alloc(t):
+            if ("o", t) not in st:
+                st[("o", t)] = epi_box[0].tile([P, N], F32, tag="o", name="o", bufs=4)
+            return st[("o", t)]
+
+        def np_g(t):
+            if not okt(t) or NP_SPLIT == 0:
+                return
+            o = np_alloc(t)
+            nc.gpsimd.tensor_tensor(
+                out=o[:, 0:NP_SPLIT], in0=st[("w", t)][:, 0:NP_SPLIT], in1=g_b[:, 0:NP_SPLIT], op=ALU.mult
+            )
+
+        def op_np(t):
+            if not okt(t):
+                return
+            o = np_alloc(t)
+            nc.vector.tensor_tensor(
+                out=o[:, NP_SPLIT:N], in0=st[("w", t)][:, NP_SPLIT:N], in1=g_b[:, NP_SPLIT:N], op=ALU.mult
+            )
+
+        def op_o(t):
+            if not okt(t):
+                return
+            o = st[("o", t)]
+            nc.vector.scalar_tensor_tensor(
+                out=o[:], in0=o[:], scalar=st[("rs2", t)][:], in1=b_b[:], op0=ALU.mult, op1=ALU.add
+            )
+            nc.sync.dma_start(out=o0_v[:, t, :], in_=o[:])
+
         load_x(0)
+        load_x(1)
         nc.sync.dma_start(out=vec[0:8, :], in_=gate_b.rearrange("(j m) -> j m", m=P))
         nc.sync.dma_start(out=vec[8:16, :], in_=pre_gamma.rearrange("(j m) -> j m", m=P))
         nc.sync.dma_start(out=vec[16:24, :], in_=pre_beta.rearrange("(j m) -> j m", m=P))
@@ -230,7 +488,6 @@ def tile_mnelayer_pa_kernel(
                 raw = wt.tile([P, 4 * N], BF16, tag="wraw", name="graw", bufs=4)
                 nc.sync.dma_start(out=raw[:].rearrange("p (j k) -> p j k", j=4), in_=gw_v[h])
                 graw.append(raw)
-            load_x(1)
             load_pv(0)
             nc.sync.dma_start(out=g_b[:], in_=ln_gamma.partition_broadcast(P))
             nc.sync.dma_start(out=b_b[:], in_=ln_beta.partition_broadcast(P))
@@ -238,15 +495,6 @@ def tile_mnelayer_pa_kernel(
                 load_x(q)
                 load_pv(q - 1)
             load_pv(NQ - 1)
-
-            vbank = ps.tile([P, P], BF16, tag="tin", name="vbank")
-            nc.tensor.transpose(out=vbank[:], in_=vec[:], identity=idb[:])
-            nc.vector.tensor_copy(out=vT[:, 0:24], in_=vbank[:, 0:24])
-
-            xT_pe(0)
-            xT_exit(0)
-            stats_a(0)
-            stats_b(0)
 
             def syn_prep(c):
                 grps = []
@@ -265,12 +513,6 @@ def tile_mnelayer_pa_kernel(
                         out=sc[:, o : o + 512].bitcast(FP8X4), scales=ss[:, o : o + 512], in_=grps[h][:]
                     )
 
-            syn_prep(0)
-            q_x(0)
-            z_c(0)
-            syn_prep(1)
-            zT_e(0)
-
             def gw_prep(h):
                 gww = graw[h][:].bitcast(F32)
                 grps = []
@@ -288,12 +530,10 @@ def tile_mnelayer_pa_kernel(
                                     in_=gww[:, 512 * j + 128 * b : 512 * j + 128 * b + 128],
                                     identity=idf[:],
                                 )
-                        dst = grw[:, 512 * jq : 512 * jq + 512].rearrange("p (n u) -> p n u", u=2)
-                        src = bank[:].rearrange("p (u n) -> p n u", u=2)
-                        if GW_EXIT_ON_S:
-                            nc.scalar.copy(out=dst, in_=src)
-                        else:
-                            nc.vector.tensor_copy(out=dst, in_=src)
+                        nc.scalar.copy(
+                            out=grw[:, 512 * jq : 512 * jq + 512].rearrange("p (n u) -> p n u", u=2),
+                            in_=bank[:].rearrange("p (u n) -> p n u", u=2),
+                        )
                     grps.append(grp)
                 for g in range(2):
                     o = N * g + 512 * h
@@ -301,207 +541,148 @@ def tile_mnelayer_pa_kernel(
                         out=gwc[:, o : o + 512].bitcast(FP8X4), scales=gws[:, o : o + 512], in_=grps[g][:]
                     )
 
+            st6 = sml.tile([P, 24], F32, tag="st6", name="st6", bufs=1)
+            mv = sml.tile([P, 4], F32, tag="mv", name="mv", bufs=1)
+            for ii in range(2):
+                for hh in range(2):
+                    k6 = 6 * (2 * ii + hh)
+                    nc.vector.bn_stats(
+                        out=st6[:, k6 : k6 + 6], in_=x_t[0][:, N * ii + 512 * hh : N * ii + 512 * hh + 512]
+                    )
+            for ii in range(2):
+                nc.vector.bn_aggr(out=mv[:, 2 * ii : 2 * ii + 2], in_=st6[:, 12 * ii : 12 * ii + 12])
+            mvv = mv[:].rearrange("p (i s) -> p i s", s=2)
+            nm0 = sml.tile([P, 2], F32, tag="nm", name="nm", bufs=6)
+            nc.gpsimd.tensor_scalar(out=nm0[:], in0=mvv[:, :, 0], scalar1=-1.0, scalar2=0.0, op0=ALU.mult, op1=ALU.add)
+            va0 = sml.tile([P, 2], F32, tag="va", name="va")
+            nc.gpsimd.tensor_scalar(out=va0[:], in0=mvv[:, :, 1], scalar1=1.0, scalar2=EPS, op0=ALU.mult, op1=ALU.add)
+            st[("nm", 0)] = nm0
+            st[("va", 0)] = va0
+            powx(0)
+
+            xT_pe(0)
+            dd(0)
+            vbank = ps.tile([P, P], BF16, tag="gt", name="vbank")
+            nc.tensor.transpose(out=vbank[:], in_=vec[:], identity=idb[:])
+            nc.vector.tensor_copy(out=vT[:, 0:24], in_=vbank[:, 0:24])
+            qx(0)
+            xT_pe(1)
+            dd(1)
+            pe_sum(1)
+            syn_prep(0)
+            cc(0, -1)
+            nm_s(1)
+            bb(1)
+            powx(1)
+            zT_bank(0, 0)
+            zT_bank(0, 1)
+            e_bank(0, 0)
+            zT_bank(0, 2)
+            e_bank(0, 1)
+            zT_bank(0, 3)
+            e_bank(0, 2)
+            e_bank(0, 3)
+            syn_prep(1)
+            qx(1)
+            rg(0, 0, False)
+            rg(0, 1, False)
+            qz(0)
             gw_prep(0)
-            rg_v(0)
-            rg_v(1)
-            q_z(0)
-            q_z(1)
             gw_prep(1)
+            syn_mx(0)
 
-        epi = ctx.enter_context(tc.tile_pool(name="epi", bufs=3))
+        epi_box.append(ctx.enter_context(tc.tile_pool(name="epi", bufs=3)))
 
-        def gate(q):
-            gts = epi.tile([P, 2048], F32, tag="gts", name="gts", bufs=2)
-            xc = st["xc"]
-            xs = st["xs"]
-            for jp in range(4):
-                bank = ps.tile([P, 512], F32, tag="gt", name="gtbank")
-                for jj in range(2):
-                    j = 2 * jp + jj
-                    for g in range(2):
-                        o = N * g + 128 * j
-                        nc.tensor.matmul_mx(
-                            out=bank[:, 256 * jj : 256 * jj + 256],
-                            lhsT=gwc[:, o : o + 128].bitcast(FP8X4),
-                            lhsT_scale=gws[:, o : o + 128],
-                            rhs=xc[:, 256 * g : 256 * g + 256].bitcast(FP8X4),
-                            rhs_scale=xs[:, 256 * g : 256 * g + 256],
-                            start=(g == 0),
-                            stop=(g == 1),
-                        )
-                for jj in range(2):
-                    j = 2 * jp + jj
-                    nc.scalar.activation(
-                        out=gts[:, 256 * j : 256 * j + 256],
-                        in_=bank[:, 256 * jj : 256 * jj + 256],
-                        func=ACT.Sigmoid,
-                        bias=vT[:, j : j + 1],
-                    )
-            st["gts_next"] = gts
+        gate_mx(0, 0)
+        gate_mx(0, 1)
+        h_bank(0, 0)
+        gate_mx(0, 2)
+        h_bank(0, 1)
+        gate_mx(0, 3)
+        h_bank(0, 2)
+        h_bank(0, 3)
+        gback(0)
+        op_g(0)
+        op_i(0)
+        syn_mx(1)
+        cc(1, -1)
+        op_j(0)
+        zT_bank(1, 0)
+        zT_bank(1, 1)
+        gate_mx(1, 0)
+        gate_mx(1, 1)
+        e_bank(1, 0)
+        e_bank(1, 1)
+        xT_pe(2)
+        dd(2)
+        zT_bank(1, 2)
+        zT_bank(1, 3)
 
-        ep = {}
-
-        def gback(t, gts):
-            ii = t % 2
-            banks = []
-            for h in range(2):
-                bank = ps.tile([P, 512], F32, tag="gb", name="gbbank")
-                for jj in range(4):
-                    j = 4 * h + jj
-                    nc.tensor.transpose(
-                        out=bank[:, 128 * jj : 128 * jj + 128],
-                        in_=gts[:, 256 * j + 128 * ii : 256 * j + 128 * ii + 128],
-                        identity=idf[:],
-                    )
-                banks.append(bank)
-            ep[("gb", t)] = banks
-
-        def syn_mx(t, zc, zs):
-            ii = t % 2
-            banks = []
-            for h in range(2):
-                bank = ps.tile([P, 512], F32, tag="pre", name="prebank")
-                for c in range(2):
-                    o = 256 * c + 128 * ii
-                    w = N * c + 512 * h
-                    nc.tensor.matmul_mx(
-                        out=bank[:],
-                        lhsT=zc[:, o : o + 128].bitcast(FP8X4),
-                        lhsT_scale=zs[:, o : o + 128],
-                        rhs=sc[:, w : w + 512].bitcast(FP8X4),
-                        rhs_scale=ss[:, w : w + 512],
-                        start=(c == 0),
-                        stop=(c == 1),
-                    )
-                banks.append(bank)
-            ep[("pre", t)] = banks
-
-        def xs_of(t):
-            return x_t[t // 2][:, N * (t % 2) : N * (t % 2) + N]
-
-        def op_g(t):
-            pt = epi.tile([P, N], F32, tag="p", name="pt")
-            pv = pv_t[t // 2]
-            o = N * (t % 2)
-            for h in range(2):
-                nc.vector.scalar_tensor_tensor(
-                    out=pt[:, 512 * h : 512 * h + 512],
-                    in0=pv[:, o + 512 * h : o + 512 * h + 512],
-                    scalar=DECAY,
-                    in1=ep[("pre", t)][h][:],
-                    op0=ALU.mult,
-                    op1=ALU.add,
-                )
-            nc.sync.dma_start(out=o1_v[:, t, :], in_=pt[:])
-            ep[("p", t)] = pt
-
-        def op_i(t):
-            w = epi.tile([P, N], F32, tag="w", name="w", bufs=4)
-            pt = ep[("p", t)]
-            nc.vector.scalar_tensor_tensor(out=w[:], in0=pt[:], scalar=SLOPE, in1=pt[:], op0=ALU.mult, op1=ALU.max)
-            ep[("w", t)] = w
-
-        def op_j(t):
-            w = ep[("w", t)]
-            nc.vector.tensor_tensor(out=w[:], in0=w[:], in1=xs_of(t), op=ALU.subtract)
-
-        def op_k(t):
-            w = ep[("w", t)]
-            for h in range(2):
-                nc.vector.tensor_tensor(
-                    out=w[:, 512 * h : 512 * h + 512],
-                    in0=w[:, 512 * h : 512 * h + 512],
-                    in1=ep[("gb", t)][h][:],
-                    op=ALU.mult,
-                )
-
-        def op_l(t):
-            w = ep[("w", t)]
-            sr = sml.tile([P, 1], F32, tag="sr", name="sr")
-            nc.vector.scalar_tensor_tensor(
-                out=w[:], in0=w[:], scalar=1.0, in1=xs_of(t), op0=ALU.mult, op1=ALU.add, accum_out=sr[:]
-            )
-            nm2 = sml.tile([P, 1], F32, tag="nm2", name="nm2")
-            nc.vector.tensor_scalar(out=nm2[:], in0=sr[:], scalar1=-1.0 / N, scalar2=None, op0=ALU.mult)
-            ep[("nm2", t)] = nm2
-
-        def op_m(t):
-            w = ep[("w", t)]
-            sq2 = sml.tile([P, 1], F32, tag="sq2", name="sq2")
-            junk = pro.tile([P, N], BF16, tag="junk", name="junk")
-            nc.scalar.activation(out=junk[:], in_=w[:], func=ACT.Square, bias=ep[("nm2", t)][:], accum_out=sq2[:])
-            v2 = sml.tile([P, 1], F32, tag="v2", name="v2")
-            nc.gpsimd.tensor_scalar(out=v2[:], in0=sq2[:], scalar1=1.0 / N, scalar2=EPS, op0=ALU.mult, op1=ALU.add)
-            rs2 = sml.tile([P, 1], F32, tag="rs2", name="rs2")
-            nc.gpsimd.tensor_tensor(out=rs2[:], in0=v2[:], in1=mh[:, 0:1], op=ALU.pow)
-            ep[("rs2", t)] = rs2
-
-        def op_n(t):
-            o = epi.tile([P, N], F32, tag="o", name="o")
-            nc.vector.scalar_tensor_tensor(
-                out=o[:], in0=ep[("w", t)][:], scalar=ep[("nm2", t)][:], in1=g_b[:], op0=ALU.add, op1=ALU.mult
-            )
-            ep[("o", t)] = o
-
-        def op_o(t):
-            o = ep[("o", t)]
-            nc.vector.scalar_tensor_tensor(
-                out=o[:], in0=o[:], scalar=ep[("rs2", t)][:], in1=b_b[:], op0=ALU.mult, op1=ALU.add
-            )
-            nc.sync.dma_start(out=o0_v[:, t, :], in_=o[:])
-
-        gate(0)
-        cur = {"gts": st["gts_next"], "zc": st["zc_next"], "zs": st["zs_next"]}
-        gback(0, cur["gts"])
-        xT_pe(1)
-        syn_mx(0, cur["zc"], cur["zs"])
-
-        for q in range(NQ):
-            nx = q + 1 < NQ
-            t0 = 2 * q
-            t1 = 2 * q + 1
-            if nx:
-                xT_exit(q + 1)
-            op_g(t0)
-            syn_mx(t1, cur["zc"], cur["zs"])
-            if nx:
-                stats_a(q + 1)
-            op_i(t0)
-            op_j(t0)
-            op_k(t0)
-            gback(t1, cur["gts"])
-            if nx:
-                stats_b(q + 1)
-            op_l(t0)
-            if nx:
-                q_x(q + 1)
-            op_m(t0)
-            if nx:
-                z_c(q + 1)
-            op_g(t1)
-            op_i(t1)
-            op_j(t1)
-            op_k(t1)
-            op_l(t1)
-            if nx:
-                gate(q + 1)
-            op_m(t1)
-            if nx:
-                zT_e(q + 1)
-            op_n(t0)
-            if nx:
-                rg_v(0)
-            op_o(t0)
-            if nx:
-                q_z(0)
-                rg_v(1)
-            op_n(t1)
-            if nx:
-                q_z(1)
-            op_o(t1)
-            if nx:
-                cur = {"gts": st["gts_next"], "zc": st["zc_next"], "zs": st["zs_next"]}
-                gback(t0 + 2, cur["gts"])
-                if q + 2 < NQ:
-                    xT_pe(q + 2)
-                syn_mx(t0 + 2, cur["zc"], cur["zs"])
+        for tau in range(0, NT + 2):
+            if tau % 2 == 0:
+                r = (tau + 2) // 2
+                r2 = r + 1
+                np_g(tau - 1)
+                op_m(tau - 1)
+                op_k(tau)
+                op_g(tau + 1)
+                e_bank(r, 2)
+                v2(tau - 1)
+                pow_r(tau - 1)
+                pe_sum(r2)
+                gback(tau + 1)
+                h_bank(r, 0)
+                gate_mx(r, 2)
+                op_o(tau - 2)
+                s1(tau)
+                op_i(tau + 1)
+                e_bank(r, 3)
+                if r >= 2:
+                    rg(r, 1, RG_ON_S)
+                nm_s(r2)
+                h_bank(r, 1)
+                gate_mx(r, 3)
+                op_np(tau - 1)
+                s2(tau)
+                op_j(tau + 1)
+                bb(r2)
+                if r == 1:
+                    rg(r, 0, False)
+                    rg(r, 1, False)
+                qz(r)
+                qx(r2)
+                syn_mx(tau + 2)
+                op_l(tau)
+            else:
+                r1 = (tau + 1) // 2
+                r = r1 + 1
+                r2 = r1 + 2
+                np_g(tau - 1)
+                op_m(tau - 1)
+                powx(r)
+                op_k(tau)
+                op_g(tau + 1)
+                cc(r, tau - 1)
+                pow_r(tau - 1)
+                zT_bank(r, 0)
+                zT_bank(r, 1)
+                op_o(tau - 2)
+                s1(tau)
+                op_i(tau + 1)
+                h_bank(r1, 2)
+                gate_mx(r, 0)
+                h_bank(r1, 3)
+                gate_mx(r, 1)
+                gback(tau + 1)
+                op_np(tau - 1)
+                s2(tau)
+                op_j(tau + 1)
+                e_bank(r, 0)
+                e_bank(r, 1)
+                rg(r, 0, RG_ON_S and r >= 2)
+                xT_pe(r2)
+                syn_mx(tau + 2)
+                dd(r2)
+                zT_bank(r, 2)
+                zT_bank(r, 3)
+                op_l(tau)

@@ -24,6 +24,7 @@ FLOPS = 2 * 2 * B * N * N
 MANUAL = True
 RG_ON_S = True
 NP_SPLIT = 0
+SUMW = 128
 
 
 def tile_mnelayer_pa_kernel(
@@ -55,7 +56,7 @@ def tile_mnelayer_pa_kernel(
         nc.vector.memset(vec[:], 0.0)
         d0 = res.tile([P, 1], F32, name="d0")
         nc.vector.memset(d0[:], 0.0)
-        ones = res.tile([P, 32], BF16, name="ones")
+        ones = res.tile([P, SUMW], BF16, name="ones")
         nc.vector.memset(ones[:], 1.0)
         eps_t = res.tile([P, 1], F32, name="eps_t")
         nc.vector.memset(eps_t[:], EPS)
@@ -137,13 +138,13 @@ def tile_mnelayer_pa_kernel(
         def pe_sum(r):
             if not okr(r):
                 return
-            bank = ps.tile([P, 64], F32, tag="tin", name="sbank")
+            bank = ps.tile([P, 2 * SUMW], F32, tag="tin", name="sbank")
             for ii in range(2):
                 for g in range(2):
                     xv = st[("xg", r)][g][:].rearrange("p (r t) -> p r t", t=4)
                     for t in range(4):
                         nc.tensor.matmul(
-                            out=bank[:, 32 * ii : 32 * ii + 32],
+                            out=bank[:, SUMW * ii : SUMW * ii + SUMW],
                             lhsT=xv[:, 128 * ii : 128 * ii + 128, t],
                             rhs=ones[:],
                             start=(g == 0 and t == 0),
@@ -156,7 +157,7 @@ def tile_mnelayer_pa_kernel(
                 return
             nm = sml.tile([P, 2], F32, tag="nm", name="nm", bufs=6)
             nc.scalar.mul(
-                out=nm[:], in_=st[("sbank", r)][:].rearrange("p (i c) -> p i c", c=32)[:, :, 0], mul=-1.0 / N
+                out=nm[:], in_=st[("sbank", r)][:].rearrange("p (i c) -> p i c", c=SUMW)[:, :, 0], mul=-1.0 / N
             )
             st[("nm", r)] = nm
 
@@ -183,27 +184,34 @@ def tile_mnelayer_pa_kernel(
                 return
             rs = sml.tile([P, 2], F32, tag="rs", name="rs")
             nc.gpsimd.tensor_tensor(out=rs[:], in0=st[("va", r)][:], in1=mh[:], op=ALU.pow)
+            st[("rs1", r)] = rs
+
+        def nr_s(r):
+            if not okr(r):
+                return
+            rs = st[("rs1", r)]
+            nm = st[("nm", r)]
             nr = sml.tile([P, 2], F32, tag="nr", name="nr")
-            nc.gpsimd.tensor_tensor(out=nr[:], in0=st[("nm", r)][:], in1=rs[:], op=ALU.mult)
+            for ii in range(2):
+                nc.scalar.activation(
+                    out=nr[:, ii : ii + 1], in_=nm[:, ii : ii + 1], func=ACT.Identity, scale=rs[:, ii : ii + 1]
+                )
             st[("rs", r)] = (rs, nr)
 
-        def cc(r, tv):
-            if okr(r):
-                z = pro.tile([P, 2 * N], F32, tag="z", name="z")
-                rs, nr = st[("rs", r)]
-                for ii in range(2):
-                    nc.scalar.activation(
-                        out=z[:, N * ii : N * ii + N],
-                        in_=x_t[r][:, N * ii : N * ii + N],
-                        func=ACT.Identity,
-                        scale=rs[:, ii : ii + 1],
-                        bias=nr[:, ii : ii + 1],
-                    )
-                    if ii == 0:
-                        v2(tv)
-                st[("z", r)] = z
-            else:
-                v2(tv)
+        def cc(r):
+            if not okr(r):
+                return
+            z = pro.tile([P, 2 * N], F32, tag="z", name="z")
+            rs, nr = st[("rs", r)]
+            for ii in range(2):
+                nc.scalar.activation(
+                    out=z[:, N * ii : N * ii + N],
+                    in_=x_t[r][:, N * ii : N * ii + N],
+                    func=ACT.Identity,
+                    scale=rs[:, ii : ii + 1],
+                    bias=nr[:, ii : ii + 1],
+                )
+            st[("z", r)] = z
 
         def zT_bank(r, b):
             if not okr(r):
@@ -553,12 +561,15 @@ def tile_mnelayer_pa_kernel(
                 nc.vector.bn_aggr(out=mv[:, 2 * ii : 2 * ii + 2], in_=st6[:, 12 * ii : 12 * ii + 12])
             mvv = mv[:].rearrange("p (i s) -> p i s", s=2)
             nm0 = sml.tile([P, 2], F32, tag="nm", name="nm", bufs=6)
-            nc.gpsimd.tensor_scalar(out=nm0[:], in0=mvv[:, :, 0], scalar1=-1.0, scalar2=0.0, op0=ALU.mult, op1=ALU.add)
+            nc.vector.tensor_scalar(out=nm0[:], in0=mvv[:, :, 0], scalar1=-1.0, scalar2=None, op0=ALU.mult)
             va0 = sml.tile([P, 2], F32, tag="va", name="va")
-            nc.gpsimd.tensor_scalar(out=va0[:], in0=mvv[:, :, 1], scalar1=1.0, scalar2=EPS, op0=ALU.mult, op1=ALU.add)
+            nc.vector.tensor_scalar(out=va0[:], in0=mvv[:, :, 1], scalar1=EPS, scalar2=None, op0=ALU.add)
             st[("nm", 0)] = nm0
             st[("va", 0)] = va0
             powx(0)
+            nr0 = sml.tile([P, 2], F32, tag="nr", name="nr")
+            nc.vector.tensor_tensor(out=nr0[:], in0=nm0[:], in1=st[("rs1", 0)][:], op=ALU.mult)
+            st[("rs", 0)] = (st[("rs1", 0)], nr0)
 
             xT_pe(0)
             dd(0)
@@ -570,10 +581,8 @@ def tile_mnelayer_pa_kernel(
             dd(1)
             pe_sum(1)
             syn_prep(0)
-            cc(0, -1)
+            cc(0)
             nm_s(1)
-            bb(1)
-            powx(1)
             zT_bank(0, 0)
             zT_bank(0, 1)
             e_bank(0, 0)
@@ -589,6 +598,7 @@ def tile_mnelayer_pa_kernel(
             qz(0)
             gw_prep(0)
             gw_prep(1)
+            bb(1)
             syn_mx(0)
 
         epi_box.append(ctx.enter_context(tc.tile_pool(name="epi", bufs=3)))
@@ -605,7 +615,9 @@ def tile_mnelayer_pa_kernel(
         op_g(0)
         op_i(0)
         syn_mx(1)
-        cc(1, -1)
+        powx(1)
+        nr_s(1)
+        cc(1)
         op_j(0)
         zT_bank(1, 0)
         zT_bank(1, 1)
@@ -622,58 +634,60 @@ def tile_mnelayer_pa_kernel(
             if tau % 2 == 0:
                 r = (tau + 2) // 2
                 r2 = r + 1
+                pow_r(tau - 2)
                 np_g(tau - 1)
                 op_m(tau - 1)
                 op_k(tau)
                 op_g(tau + 1)
                 e_bank(r, 2)
-                v2(tau - 1)
-                pow_r(tau - 1)
                 pe_sum(r2)
                 gback(tau + 1)
-                h_bank(r, 0)
-                gate_mx(r, 2)
-                op_o(tau - 2)
-                s1(tau)
-                op_i(tau + 1)
                 e_bank(r, 3)
                 if r >= 2:
                     rg(r, 1, RG_ON_S)
-                nm_s(r2)
+                v2(tau - 1)
+                op_o(tau - 2)
+                s1(tau)
+                op_i(tau + 1)
+                h_bank(r, 0)
+                gate_mx(r, 2)
                 h_bank(r, 1)
                 gate_mx(r, 3)
-                op_np(tau - 1)
-                s2(tau)
-                op_j(tau + 1)
-                bb(r2)
                 if r == 1:
                     rg(r, 0, False)
                     rg(r, 1, False)
                 qz(r)
-                qx(r2)
                 syn_mx(tau + 2)
+                op_np(tau - 1)
+                s2(tau)
+                op_j(tau + 1)
+                nm_s(r2)
+                bb(r2)
+                qx(r2)
                 op_l(tau)
             else:
                 r1 = (tau + 1) // 2
                 r = r1 + 1
                 r2 = r1 + 2
+                pow_r(tau - 2)
+                powx(r)
                 np_g(tau - 1)
                 op_m(tau - 1)
-                powx(r)
                 op_k(tau)
                 op_g(tau + 1)
-                cc(r, tau - 1)
-                pow_r(tau - 1)
-                zT_bank(r, 0)
-                zT_bank(r, 1)
-                op_o(tau - 2)
-                s1(tau)
-                op_i(tau + 1)
                 h_bank(r1, 2)
+                v2(tau - 1)
                 gate_mx(r, 0)
                 h_bank(r1, 3)
                 gate_mx(r, 1)
                 gback(tau + 1)
+                op_o(tau - 2)
+                s1(tau)
+                op_i(tau + 1)
+                nr_s(r)
+                cc(r)
+                zT_bank(r, 0)
+                zT_bank(r, 1)
                 op_np(tau - 1)
                 s2(tau)
                 op_j(tau + 1)

@@ -25,6 +25,8 @@ MANUAL = True
 RG_ON_S = True
 NP_SPLIT = 0
 SUMW = 128
+EARLY_POW = 11
+TAIL_S = (11, 12, 13)
 
 
 def tile_mnelayer_pa_kernel(
@@ -71,7 +73,7 @@ def tile_mnelayer_pa_kernel(
         ss = res.tile([P, 2 * N], U8, name="ss", align_bytes=64)
         gwc = res.tile([P, 2 * N], U32, name="gwc", align_bytes=64)
         gws = res.tile([P, 2 * N], U8, name="gws", align_bytes=64)
-        vT = res.tile([P, 32], F32, name="vT")
+        vT = res.tile([P, 40], F32, name="vT")
 
         def load_x(q):
             nc.sync.dma_start(out=x_t[q][:].rearrange("p (i k) -> p i k", i=2), in_=x_v[:, 2 * q : 2 * q + 2, :])
@@ -464,15 +466,64 @@ def tile_mnelayer_pa_kernel(
             )
 
         def op_np(t):
-            if not okt(t):
+            if not okt(t) or t in TAIL_S:
                 return
             o = np_alloc(t)
             nc.vector.tensor_tensor(
                 out=o[:, NP_SPLIT:N], in0=st[("w", t)][:, NP_SPLIT:N], in1=g_b[:, NP_SPLIT:N], op=ALU.mult
             )
 
+        def tail_a(t):
+            if t not in TAIL_S:
+                return
+            t1 = epi_box[0].tile([P, N], F32, tag="tl", name="t1", bufs=5)
+            nc.scalar.activation(out=t1[:], in_=st[("w", t)][:], func=ACT.Identity, scale=st[("rs2", t)][:])
+            banks = []
+            for h in range(2):
+                bank = ps.tile([P, 512], F32, tag="tin", name="tbank")
+                for jj in range(4):
+                    j = 4 * h + jj
+                    nc.tensor.transpose(
+                        out=bank[:, 128 * jj : 128 * jj + 128], in_=t1[:, 128 * j : 128 * j + 128], identity=idf[:]
+                    )
+                banks.append(bank)
+            st[("tbank", t)] = banks
+
+        def tail_b(t):
+            if t not in TAIL_S:
+                return
+            oT = epi_box[0].tile([P, N], F32, tag="tl", name="oT", bufs=5)
+            for h in range(2):
+                for jj in range(4):
+                    j = 4 * h + jj
+                    nc.scalar.activation(
+                        out=oT[:, 128 * j : 128 * j + 128],
+                        in_=st[("tbank", t)][h][:, 128 * jj : 128 * jj + 128],
+                        func=ACT.Identity,
+                        scale=vT[:, 24 + j : 25 + j],
+                        bias=vT[:, 32 + j : 33 + j],
+                    )
+            banks = []
+            for h in range(2):
+                bank = ps.tile([P, 512], F32, tag="gt", name="ubank")
+                for jj in range(4):
+                    j = 4 * h + jj
+                    nc.tensor.transpose(
+                        out=bank[:, 128 * jj : 128 * jj + 128], in_=oT[:, 128 * j : 128 * j + 128], identity=idf[:]
+                    )
+                banks.append(bank)
+            st[("ubank", t)] = banks
+
+        def tail_c(t):
+            if t not in TAIL_S:
+                return
+            of = epi_box[0].tile([P, N], F32, tag="tl", name="of", bufs=5)
+            for h in range(2):
+                nc.scalar.copy(out=of[:, 512 * h : 512 * h + 512], in_=st[("ubank", t)][h][:])
+            nc.sync.dma_start(out=o0_v[:, t, :], in_=of[:])
+
         def op_o(t):
-            if not okt(t):
+            if not okt(t) or t in TAIL_S:
                 return
             o = st[("o", t)]
             nc.vector.scalar_tensor_tensor(
@@ -485,6 +536,8 @@ def tile_mnelayer_pa_kernel(
         nc.sync.dma_start(out=vec[0:8, :], in_=gate_b.rearrange("(j m) -> j m", m=P))
         nc.sync.dma_start(out=vec[8:16, :], in_=pre_gamma.rearrange("(j m) -> j m", m=P))
         nc.sync.dma_start(out=vec[16:24, :], in_=pre_beta.rearrange("(j m) -> j m", m=P))
+        nc.sync.dma_start(out=vec[24:32, :], in_=ln_gamma.rearrange("(j m) -> j m", m=P))
+        nc.sync.dma_start(out=vec[32:40, :], in_=ln_beta.rearrange("(j m) -> j m", m=P))
         with tc.tile_pool(name="wt", bufs=1) as wt:
             sraw = []
             for c in range(2):
@@ -575,7 +628,7 @@ def tile_mnelayer_pa_kernel(
             dd(0)
             vbank = ps.tile([P, P], BF16, tag="gt", name="vbank")
             nc.tensor.transpose(out=vbank[:], in_=vec[:], identity=idb[:])
-            nc.vector.tensor_copy(out=vT[:, 0:24], in_=vbank[:, 0:24])
+            nc.vector.tensor_copy(out=vT[:, 0:40], in_=vbank[:, 0:40])
             qx(0)
             xT_pe(1)
             dd(1)
@@ -630,15 +683,17 @@ def tile_mnelayer_pa_kernel(
         zT_bank(1, 2)
         zT_bank(1, 3)
 
-        for tau in range(0, NT + 2):
+        for tau in range(0, NT - 2):
             if tau % 2 == 0:
                 r = (tau + 2) // 2
                 r2 = r + 1
-                pow_r(tau - 2)
+                if tau - 2 < EARLY_POW:
+                    pow_r(tau - 2)
                 np_g(tau - 1)
                 op_m(tau - 1)
                 op_k(tau)
                 op_g(tau + 1)
+                tail_b(tau - 2)
                 e_bank(r, 2)
                 pe_sum(r2)
                 gback(tau + 1)
@@ -646,9 +701,12 @@ def tile_mnelayer_pa_kernel(
                 if r >= 2:
                     rg(r, 1, RG_ON_S)
                 v2(tau - 1)
+                if tau - 1 >= EARLY_POW:
+                    pow_r(tau - 1)
                 op_o(tau - 2)
                 s1(tau)
                 op_i(tau + 1)
+                tail_c(tau - 2)
                 h_bank(r, 0)
                 gate_mx(r, 2)
                 h_bank(r, 1)
@@ -663,13 +721,15 @@ def tile_mnelayer_pa_kernel(
                 op_j(tau + 1)
                 nm_s(r2)
                 bb(r2)
+                tail_a(tau - 1)
                 qx(r2)
                 op_l(tau)
             else:
                 r1 = (tau + 1) // 2
                 r = r1 + 1
                 r2 = r1 + 2
-                pow_r(tau - 2)
+                if tau - 2 < EARLY_POW:
+                    pow_r(tau - 2)
                 powx(r)
                 np_g(tau - 1)
                 op_m(tau - 1)
@@ -677,10 +737,13 @@ def tile_mnelayer_pa_kernel(
                 op_g(tau + 1)
                 h_bank(r1, 2)
                 v2(tau - 1)
+                if tau - 1 >= EARLY_POW:
+                    pow_r(tau - 1)
                 gate_mx(r, 0)
                 h_bank(r1, 3)
                 gate_mx(r, 1)
                 gback(tau + 1)
+                tail_b(tau - 2)
                 op_o(tau - 2)
                 s1(tau)
                 op_i(tau + 1)
@@ -694,9 +757,44 @@ def tile_mnelayer_pa_kernel(
                 e_bank(r, 0)
                 e_bank(r, 1)
                 rg(r, 0, RG_ON_S and r >= 2)
+                tail_c(tau - 2)
                 xT_pe(r2)
                 syn_mx(tau + 2)
                 dd(r2)
                 zT_bank(r, 2)
                 zT_bank(r, 3)
+                tail_a(tau - 1)
                 op_l(tau)
+
+        op_m(13)
+        op_k(14)
+        gback(15)
+        op_g(15)
+        v2(13)
+        pow_r(13)
+        tail_b(12)
+        s1(14)
+        op_i(15)
+        tail_a(13)
+        tail_c(12)
+        s2(14)
+        op_j(15)
+        op_l(14)
+
+        op_m(14)
+        op_k(15)
+        v2(14)
+        pow_r(14)
+        tail_b(13)
+        s1(15)
+        op_np(14)
+        s2(15)
+        op_l(15)
+
+        op_m(15)
+        op_np(15)
+        v2(15)
+        pow_r(15)
+        op_o(14)
+        tail_c(13)
+        op_o(15)

@@ -56,6 +56,11 @@ def tile_mnelayer_pa_kernel(
         nc.gpsimd.memset(mh[:], -0.5)
         vec = res.tile([P, P], BF16, name="vec")
         nc.vector.memset(vec[:], 0.0)
+        nc.scalar.dma_start(out=vec[0:8, :], in_=gate_b.rearrange("(j m) -> j m", m=P))
+        nc.scalar.dma_start(out=vec[8:16, :], in_=pre_gamma.rearrange("(j m) -> j m", m=P))
+        nc.scalar.dma_start(out=vec[16:24, :], in_=pre_beta.rearrange("(j m) -> j m", m=P))
+        nc.scalar.dma_start(out=vec[24:32, :], in_=ln_gamma.rearrange("(j m) -> j m", m=P))
+        nc.scalar.dma_start(out=vec[32:40, :], in_=ln_beta.rearrange("(j m) -> j m", m=P))
         d0 = res.tile([P, 1], F32, name="d0")
         nc.vector.memset(d0[:], 0.0)
         ones = res.tile([P, SUMW], BF16, name="ones")
@@ -533,11 +538,6 @@ def tile_mnelayer_pa_kernel(
 
         load_x(0)
         load_x(1)
-        nc.sync.dma_start(out=vec[0:8, :], in_=gate_b.rearrange("(j m) -> j m", m=P))
-        nc.sync.dma_start(out=vec[8:16, :], in_=pre_gamma.rearrange("(j m) -> j m", m=P))
-        nc.sync.dma_start(out=vec[16:24, :], in_=pre_beta.rearrange("(j m) -> j m", m=P))
-        nc.sync.dma_start(out=vec[24:32, :], in_=ln_gamma.rearrange("(j m) -> j m", m=P))
-        nc.sync.dma_start(out=vec[32:40, :], in_=ln_beta.rearrange("(j m) -> j m", m=P))
         with tc.tile_pool(name="wt", bufs=1) as wt:
             sraw = []
             for c in range(2):
@@ -550,9 +550,13 @@ def tile_mnelayer_pa_kernel(
                 nc.sync.dma_start(out=raw[:].rearrange("p (j k) -> p j k", j=4), in_=gw_v[h])
                 graw.append(raw)
             load_pv(0)
+            load_x(2)
             nc.sync.dma_start(out=g_b[:], in_=ln_gamma.partition_broadcast(P))
+            load_pv(1)
+            load_x(3)
             nc.sync.dma_start(out=b_b[:], in_=ln_beta.partition_broadcast(P))
-            for q in range(2, NQ):
+            load_pv(2)
+            for q in range(4, NQ):
                 load_x(q)
                 load_pv(q - 1)
             load_pv(NQ - 1)
@@ -560,7 +564,7 @@ def tile_mnelayer_pa_kernel(
             def syn_prep(c):
                 grps = []
                 for h in range(2):
-                    grp = wt.tile([P, 2048], BF16, tag="wgrp", name="sgrp", bufs=3, align_bytes=64)
+                    grp = wt.tile([P, 2048], BF16, tag="wgrp", name="sgrp", bufs=6, align_bytes=64)
                     nc.vector.tensor_copy(
                         out=grp[:].rearrange("p (a i t) -> p a t i", i=4, t=4),
                         in_=sraw[c][:].rearrange("p (t n) -> p t n", t=4)[:, :, 512 * h : 512 * h + 512].rearrange(
@@ -578,7 +582,7 @@ def tile_mnelayer_pa_kernel(
                 gww = graw[h][:].bitcast(F32)
                 grps = []
                 for g in range(2):
-                    grp = wt.tile([P, 2048], BF16, tag="wgrp", name="ggrp", bufs=3, align_bytes=64)
+                    grp = wt.tile([P, 2048], BF16, tag="wgrp", name="ggrp", bufs=6, align_bytes=64)
                     grw = grp[:].bitcast(F32)
                     for jq in range(2):
                         bank = ps.tile([P, 512], F32, tag="tin", name="gbank")

@@ -56,11 +56,6 @@ def tile_mnelayer_pa_kernel(
         nc.gpsimd.memset(mh[:], -0.5)
         vec = res.tile([P, P], BF16, name="vec")
         nc.vector.memset(vec[:], 0.0)
-        nc.scalar.dma_start(out=vec[0:8, :], in_=gate_b.rearrange("(j m) -> j m", m=P))
-        nc.scalar.dma_start(out=vec[8:16, :], in_=pre_gamma.rearrange("(j m) -> j m", m=P))
-        nc.scalar.dma_start(out=vec[16:24, :], in_=pre_beta.rearrange("(j m) -> j m", m=P))
-        nc.scalar.dma_start(out=vec[24:32, :], in_=ln_gamma.rearrange("(j m) -> j m", m=P))
-        nc.scalar.dma_start(out=vec[32:40, :], in_=ln_beta.rearrange("(j m) -> j m", m=P))
         d0 = res.tile([P, 1], F32, name="d0")
         nc.vector.memset(d0[:], 0.0)
         ones = res.tile([P, SUMW], BF16, name="ones")
@@ -463,7 +458,7 @@ def tile_mnelayer_pa_kernel(
             return st[("o", t)]
 
         def np_g(t):
-            if not okt(t) or NP_SPLIT == 0:
+            if not okt(t) or NP_SPLIT == 0 or t in TAIL_S:
                 return
             o = np_alloc(t)
             nc.gpsimd.tensor_tensor(
@@ -538,6 +533,11 @@ def tile_mnelayer_pa_kernel(
 
         load_x(0)
         load_x(1)
+        nc.sync.dma_start(out=vec[0:8, :], in_=gate_b.rearrange("(j m) -> j m", m=P))
+        nc.sync.dma_start(out=vec[8:16, :], in_=pre_gamma.rearrange("(j m) -> j m", m=P))
+        nc.sync.dma_start(out=vec[16:24, :], in_=pre_beta.rearrange("(j m) -> j m", m=P))
+        nc.sync.dma_start(out=vec[24:32, :], in_=ln_gamma.rearrange("(j m) -> j m", m=P))
+        nc.sync.dma_start(out=vec[32:40, :], in_=ln_beta.rearrange("(j m) -> j m", m=P))
         with tc.tile_pool(name="wt", bufs=1) as wt:
             sraw = []
             for c in range(2):
@@ -550,13 +550,9 @@ def tile_mnelayer_pa_kernel(
                 nc.sync.dma_start(out=raw[:].rearrange("p (j k) -> p j k", j=4), in_=gw_v[h])
                 graw.append(raw)
             load_pv(0)
-            load_x(2)
             nc.sync.dma_start(out=g_b[:], in_=ln_gamma.partition_broadcast(P))
-            load_pv(1)
-            load_x(3)
             nc.sync.dma_start(out=b_b[:], in_=ln_beta.partition_broadcast(P))
-            load_pv(2)
-            for q in range(4, NQ):
+            for q in range(2, NQ):
                 load_x(q)
                 load_pv(q - 1)
             load_pv(NQ - 1)
@@ -715,14 +711,14 @@ def tile_mnelayer_pa_kernel(
                 gate_mx(r, 2)
                 h_bank(r, 1)
                 gate_mx(r, 3)
+                op_np(tau - 1)
+                s2(tau)
+                op_j(tau + 1)
                 if r == 1:
                     rg(r, 0, False)
                     rg(r, 1, False)
                 qz(r)
                 syn_mx(tau + 2)
-                op_np(tau - 1)
-                s2(tau)
-                op_j(tau + 1)
                 nm_s(r2)
                 bb(r2)
                 tail_a(tau - 1)
@@ -785,6 +781,7 @@ def tile_mnelayer_pa_kernel(
         op_j(15)
         op_l(14)
 
+        np_g(14)
         op_m(14)
         op_k(15)
         v2(14)
@@ -795,6 +792,7 @@ def tile_mnelayer_pa_kernel(
         s2(15)
         op_l(15)
 
+        np_g(15)
         op_m(15)
         op_np(15)
         v2(15)

@@ -23,7 +23,7 @@ FLOPS = 2 * 2 * B * N * N
 
 MANUAL = True
 RG_ON_S = True
-NP_SPLIT = 0
+NP_SPLIT = 384
 SUMW = 128
 EARLY_POW = 11
 TAIL_S = (11, 12, 13)

@@ -23,8 +23,9 @@ FLOPS = 2 * 2 * B * N * N
 
 MANUAL = True
 RG_ON_S = True
-NP_SPLIT = 384
+NP_BY_PARITY = (512, 768)
 SUMW = 128
+RG1_ON_S = False
 EARLY_POW = 11
 TAIL_S = (11, 12, 13)
 
@@ -458,20 +459,18 @@ def tile_mnelayer_pa_kernel(
             return st[("o", t)]
 
         def np_g(t):
-            if not okt(t) or NP_SPLIT == 0 or t in TAIL_S:
+            if not okt(t) or t in TAIL_S:
                 return
             o = np_alloc(t)
-            nc.gpsimd.tensor_tensor(
-                out=o[:, 0:NP_SPLIT], in0=st[("w", t)][:, 0:NP_SPLIT], in1=g_b[:, 0:NP_SPLIT], op=ALU.mult
-            )
+            sp = NP_BY_PARITY[t % 2]
+            nc.gpsimd.tensor_tensor(out=o[:, 0:sp], in0=st[("w", t)][:, 0:sp], in1=g_b[:, 0:sp], op=ALU.mult)
 
         def op_np(t):
             if not okt(t) or t in TAIL_S:
                 return
             o = np_alloc(t)
-            nc.vector.tensor_tensor(
-                out=o[:, NP_SPLIT:N], in0=st[("w", t)][:, NP_SPLIT:N], in1=g_b[:, NP_SPLIT:N], op=ALU.mult
-            )
+            sp = NP_BY_PARITY[t % 2]
+            nc.vector.tensor_tensor(out=o[:, sp:N], in0=st[("w", t)][:, sp:N], in1=g_b[:, sp:N], op=ALU.mult)
 
         def tail_a(t):
             if t not in TAIL_S:
@@ -698,8 +697,8 @@ def tile_mnelayer_pa_kernel(
                 pe_sum(r2)
                 gback(tau + 1)
                 e_bank(r, 3)
-                if r >= 2:
-                    rg(r, 1, RG_ON_S)
+                if r >= 2 and RG1_ON_S:
+                    rg(r, 1, True)
                 v2(tau - 1)
                 if tau - 1 >= EARLY_POW:
                     pow_r(tau - 1)
@@ -716,6 +715,7 @@ def tile_mnelayer_pa_kernel(
                 op_j(tau + 1)
                 if r == 1:
                     rg(r, 0, False)
+                if r == 1 or not RG1_ON_S:
                     rg(r, 1, False)
                 qz(r)
                 syn_mx(tau + 2)
@@ -735,6 +735,7 @@ def tile_mnelayer_pa_kernel(
                 op_m(tau - 1)
                 op_k(tau)
                 op_g(tau + 1)
+                syn_mx(tau + 2)
                 h_bank(r1, 2)
                 v2(tau - 1)
                 if tau - 1 >= EARLY_POW:
@@ -759,7 +760,6 @@ def tile_mnelayer_pa_kernel(
                 rg(r, 0, RG_ON_S and r >= 2)
                 tail_c(tau - 2)
                 xT_pe(r2)
-                syn_mx(tau + 2)
                 dd(r2)
                 zT_bank(r, 2)
                 zT_bank(r, 3)

@@ -84,6 +84,7 @@ def tile_mnelayer_pa_kernel(
 
         st = {}
         epi_box = []
+        w_box = []
 
         def okr(r):
             return 0 <= r < NQ
@@ -115,45 +116,39 @@ def tile_mnelayer_pa_kernel(
         def dd(r):
             if not okr(r):
                 return
-            tiles = []
+            xg = pro.tile([P, 2048], BF16, tag="xg", name="xg", align_bytes=64, bufs=3)
             for g in range(2):
-                xg = pro.tile([P, 1024], BF16, tag="xg", name="xg", align_bytes=64, bufs=4)
                 nc.scalar.copy(
-                    out=xg[:].bitcast(F32).rearrange("p (r u) -> p r u", u=2),
+                    out=xg[:, 1024 * g : 1024 * g + 1024].bitcast(F32).rearrange("p (r u) -> p r u", u=2),
                     in_=st[("xbank", r)][g][:].rearrange("p (u r) -> p r u", u=2),
                 )
-                tiles.append(xg)
-            st[("xg", r)] = tiles
+            st[("xg", r)] = [xg[:, 1024 * g : 1024 * g + 1024] for g in range(2)]
+            st[("xgt", r)] = xg
 
         def qx(r):
             if not okr(r):
                 return
             xc = pro.tile([P, 512], U32, tag="xc", name="xc", align_bytes=64)
             xs = pro.tile([P, 512], U8, tag="xs", name="xs", align_bytes=64)
-            for g in range(2):
-                nc.vector.quantize_mx(
-                    out=xc[:, 256 * g : 256 * g + 256].bitcast(FP8X4),
-                    scales=xs[:, 256 * g : 256 * g + 256],
-                    in_=st[("xg", r)][g][:],
-                )
+            nc.vector.quantize_mx(out=xc[:].bitcast(FP8X4), scales=xs[:], in_=st[("xgt", r)][:])
             st[("xc", r)] = (xc, xs)
 
-        def pe_sum(r):
+        def pe_sum(r, ii):
             if not okr(r):
                 return
-            bank = ps.tile([P, 2 * SUMW], F32, tag="tin", name="sbank")
-            for ii in range(2):
-                for g in range(2):
-                    xv = st[("xg", r)][g][:].rearrange("p (r t) -> p r t", t=4)
-                    for t in range(4):
-                        nc.tensor.matmul(
-                            out=bank[:, SUMW * ii : SUMW * ii + SUMW],
-                            lhsT=xv[:, 128 * ii : 128 * ii + 128, t],
-                            rhs=ones[:],
-                            start=(g == 0 and t == 0),
-                            stop=(g == 1 and t == 3),
-                        )
-            st[("sbank", r)] = bank
+            if ii == 0:
+                st[("sbank", r)] = ps.tile([P, 2 * SUMW], F32, tag="tin", name="sbank")
+            bank = st[("sbank", r)]
+            for g in range(2):
+                xv = st[("xg", r)][g].rearrange("p (r t) -> p r t", t=4)
+                for t in range(4):
+                    nc.tensor.matmul(
+                        out=bank[:, SUMW * ii : SUMW * ii + SUMW],
+                        lhsT=xv[:, 128 * ii : 128 * ii + 128, t],
+                        rhs=ones[:],
+                        start=(g == 0 and t == 0),
+                        stop=(g == 1 and t == 3),
+                    )
 
         def nm_s(r):
             if not okr(r):
@@ -164,22 +159,26 @@ def tile_mnelayer_pa_kernel(
             )
             st[("nm", r)] = nm
 
-        def bb(r):
+        def bb(r, ii):
             if not okr(r):
                 return
             nm = st[("nm", r)]
-            sq = sml.tile([P, 2], F32, tag="sq", name="sq")
-            for ii in range(2):
-                junk = pro.tile([P, N], BF16, tag="junk", name="junk")
-                nc.scalar.activation(
-                    out=junk[:],
-                    in_=x_t[r][:, N * ii : N * ii + N],
-                    func=ACT.Square,
-                    bias=nm[:, ii : ii + 1],
-                    accum_out=sq[:, ii : ii + 1],
-                )
+            if ii == 0:
+                st[("sq", r)] = sml.tile([P, 2], F32, tag="sq", name="sq")
+            junk = pro.tile([P, N + 2], BF16, tag="junk", name="junk")
+            nc.scalar.activation(
+                out=junk[:, 0:N],
+                in_=x_t[r][:, N * ii : N * ii + N],
+                func=ACT.Square,
+                bias=nm[:, ii : ii + 1],
+                accum_out=st[("sq", r)][:, ii : ii + 1],
+            )
+
+        def va_s(r):
+            if not okr(r):
+                return
             va = sml.tile([P, 2], F32, tag="va", name="va")
-            nc.scalar.activation(out=va[:], in_=sq[:], func=ACT.Identity, scale=1.0 / N, bias=eps_t[:])
+            nc.scalar.activation(out=va[:], in_=st[("sq", r)][:], func=ACT.Identity, scale=1.0 / N, bias=eps_t[:])
             st[("va", r)] = va
 
         def powx(r):
@@ -201,20 +200,22 @@ def tile_mnelayer_pa_kernel(
                 )
             st[("rs", r)] = (rs, nr)
 
-        def cc(r):
+        def cc(r, ii, on_v=False):
             if not okr(r):
                 return
-            z = pro.tile([P, 2 * N], F32, tag="z", name="z")
+            if ii == 0:
+                st[("z", r)] = pro.tile([P, 2 * N], F32, tag="z", name="z")
+            z = st[("z", r)][:, N * ii : N * ii + N]
+            x = x_t[r][:, N * ii : N * ii + N]
             rs, nr = st[("rs", r)]
-            for ii in range(2):
-                nc.scalar.activation(
-                    out=z[:, N * ii : N * ii + N],
-                    in_=x_t[r][:, N * ii : N * ii + N],
-                    func=ACT.Identity,
-                    scale=rs[:, ii : ii + 1],
-                    bias=nr[:, ii : ii + 1],
+            if on_v:
+                nc.vector.tensor_scalar(
+                    out=z, in0=x, scalar1=rs[:, ii : ii + 1], scalar2=nr[:, ii : ii + 1], op0=ALU.mult, op1=ALU.add
                 )
-            st[("z", r)] = z
+            else:
+                nc.scalar.activation(
+                    out=z, in_=x, func=ACT.Identity, scale=rs[:, ii : ii + 1], bias=nr[:, ii : ii + 1]
+                )
 
         def zT_bank(r, b):
             if not okr(r):
@@ -253,26 +254,21 @@ def tile_mnelayer_pa_kernel(
         def rg(r, c, on_s):
             if not okr(r):
                 return
-            zg = pro.tile([P, 1024], BF16, tag="zg", name="zg", align_bytes=64)
+            if c == 0:
+                st[("zg", r)] = pro.tile([P, 2048], BF16, tag="zg", name="zg", align_bytes=64)
             src = st[("zp", r, c)][:].rearrange("p (t a i) -> p a t i", t=4, i=4)
-            dst = zg[:].rearrange("p (a i t) -> p a t i", i=4, t=4)
+            dst = st[("zg", r)][:, 1024 * c : 1024 * c + 1024].rearrange("p (a i t) -> p a t i", i=4, t=4)
             if on_s:
                 nc.scalar.copy(out=dst, in_=src)
             else:
                 nc.vector.tensor_copy(out=dst, in_=src)
-            st[("zg", r, c)] = zg
 
         def qz(r):
             if not okr(r):
                 return
             zc = pro.tile([P, 512], U32, tag="zc", name="zc", align_bytes=64)
             zs = pro.tile([P, 512], U8, tag="zs", name="zs", align_bytes=64)
-            for c in range(2):
-                nc.vector.quantize_mx(
-                    out=zc[:, 256 * c : 256 * c + 256].bitcast(FP8X4),
-                    scales=zs[:, 256 * c : 256 * c + 256],
-                    in_=st[("zg", r, c)][:],
-                )
+            nc.vector.quantize_mx(out=zc[:].bitcast(FP8X4), scales=zs[:], in_=st[("zg", r)][:])
             st[("zc", r)] = (zc, zs)
 
         def gate_mx(r, b):
@@ -329,28 +325,25 @@ def tile_mnelayer_pa_kernel(
                 banks.append(bank)
             st[("gb", t)] = banks
 
-        def syn_mx(t):
+        def syn_mx(t, h):
             if not okt(t):
                 return
             zc, zs = st[("zc", t // 2)]
             ii = t % 2
-            banks = []
-            for h in range(2):
-                bank = ps.tile([P, 512], F32, tag="pre", name="prebank")
-                for c in range(2):
-                    o = 256 * c + 128 * ii
-                    w = N * c + 512 * h
-                    nc.tensor.matmul_mx(
-                        out=bank[:],
-                        lhsT=zc[:, o : o + 128].bitcast(FP8X4),
-                        lhsT_scale=zs[:, o : o + 128],
-                        rhs=sc[:, w : w + 512].bitcast(FP8X4),
-                        rhs_scale=ss[:, w : w + 512],
-                        start=(c == 0),
-                        stop=(c == 1),
-                    )
-                banks.append(bank)
-            st[("pre", t)] = banks
+            bank = ps.tile([P, 512], F32, tag="pre", name="prebank")
+            for c in range(2):
+                o = 256 * c + 128 * ii
+                w = N * c + 512 * h
+                nc.tensor.matmul_mx(
+                    out=bank[:],
+                    lhsT=zc[:, o : o + 128].bitcast(FP8X4),
+                    lhsT_scale=zs[:, o : o + 128],
+                    rhs=sc[:, w : w + 512].bitcast(FP8X4),
+                    rhs_scale=ss[:, w : w + 512],
+                    start=(c == 0),
+                    stop=(c == 1),
+                )
+            st[("pre", t, h)] = bank
 
         def op_g(t):
             if not okt(t):
@@ -363,7 +356,7 @@ def tile_mnelayer_pa_kernel(
                     out=pt[:, 512 * h : 512 * h + 512],
                     in0=pv[:, o + 512 * h : o + 512 * h + 512],
                     scalar=DECAY,
-                    in1=st[("pre", t)][h][:],
+                    in1=st[("pre", t, h)][:],
                     op0=ALU.mult,
                     op1=ALU.add,
                 )
@@ -373,16 +366,16 @@ def tile_mnelayer_pa_kernel(
         def op_i(t):
             if not okt(t):
                 return
-            w = epi_box[0].tile([P, N], F32, tag="w", name="w", bufs=4)
+            w = w_box[t % 4]
             pt = st[("p", t)]
-            nc.vector.scalar_tensor_tensor(out=w[:], in0=pt[:], scalar=SLOPE, in1=pt[:], op0=ALU.mult, op1=ALU.max)
+            nc.vector.scalar_tensor_tensor(out=w[:, 0:N], in0=pt[:], scalar=SLOPE, in1=pt[:], op0=ALU.mult, op1=ALU.max)
             st[("w", t)] = w
 
         def op_j(t):
             if not okt(t):
                 return
             w = st[("w", t)]
-            nc.vector.tensor_tensor(out=w[:], in0=w[:], in1=x_of(t), op=ALU.subtract)
+            nc.vector.tensor_tensor(out=w[:, 0:N], in0=w[:, 0:N], in1=x_of(t), op=ALU.subtract)
 
         def op_k(t):
             if not okt(t):
@@ -428,29 +421,24 @@ def tile_mnelayer_pa_kernel(
                 return
             w = st[("w", t)]
             nc.vector.scalar_tensor_tensor(
-                out=w[:], in0=w[:], scalar=st[("nmc", t)][:], in1=x_of(t), op0=ALU.add, op1=ALU.add
+                out=w[:, 0:N], in0=w[:, 0:N], scalar=st[("nmc", t)][:], in1=x_of(t), op0=ALU.add, op1=ALU.add
             )
 
         def op_m(t):
             if not okt(t):
                 return
             sq2 = sml.tile([P, 1], F32, tag="sq2", name="sq2")
-            junk = pro.tile([P, N], BF16, tag="junk", name="junk")
-            nc.scalar.activation(out=junk[:], in_=st[("w", t)][:], func=ACT.Square, accum_out=sq2[:])
+            junk = pro.tile([P, N + 2], BF16, tag="junk", name="junk")
+            nc.scalar.activation(
+                out=junk[:, 0 : N + 1], in_=st[("w", t)][:, 0 : N + 1], func=ACT.Square, scale=1.0 / 32, accum_out=sq2[:]
+            )
             st[("sq2", t)] = sq2
-
-        def v2(t):
-            if not okt(t):
-                return
-            v2t = sml.tile([P, 1], F32, tag="v2t", name="v2t")
-            nc.scalar.activation(out=v2t[:], in_=st[("sq2", t)][:], func=ACT.Identity, scale=1.0 / N, bias=eps_t[:])
-            st[("v2t", t)] = v2t
 
         def pow_r(t):
             if not okt(t):
                 return
             rs2 = sml.tile([P, 1], F32, tag="rs2", name="rs2")
-            nc.gpsimd.tensor_tensor(out=rs2[:], in0=st[("v2t", t)][:], in1=mh[:, 0:1], op=ALU.pow)
+            nc.gpsimd.tensor_tensor(out=rs2[:], in0=st[("sq2", t)][:], in1=mh[:, 0:1], op=ALU.pow)
             st[("rs2", t)] = rs2
 
         def np_alloc(t):
@@ -458,25 +446,28 @@ def tile_mnelayer_pa_kernel(
                 st[("o", t)] = epi_box[0].tile([P, N], F32, tag="o", name="o", bufs=4)
             return st[("o", t)]
 
+        def np_split(t):
+            return 0 if t == NT - 1 else NP_BY_PARITY[t % 2]
+
         def np_g(t):
             if not okt(t) or t in TAIL_S:
                 return
             o = np_alloc(t)
-            sp = NP_BY_PARITY[t % 2]
+            sp = np_split(t)
             nc.gpsimd.tensor_tensor(out=o[:, 0:sp], in0=st[("w", t)][:, 0:sp], in1=g_b[:, 0:sp], op=ALU.mult)
 
         def op_np(t):
             if not okt(t) or t in TAIL_S:
                 return
             o = np_alloc(t)
-            sp = NP_BY_PARITY[t % 2]
+            sp = np_split(t)
             nc.vector.tensor_tensor(out=o[:, sp:N], in0=st[("w", t)][:, sp:N], in1=g_b[:, sp:N], op=ALU.mult)
 
         def tail_a(t):
             if t not in TAIL_S:
                 return
             t1 = epi_box[0].tile([P, N], F32, tag="tl", name="t1", bufs=5)
-            nc.scalar.activation(out=t1[:], in_=st[("w", t)][:], func=ACT.Identity, scale=st[("rs2", t)][:])
+            nc.scalar.activation(out=t1[:], in_=st[("w", t)][:, 0:N], func=ACT.Identity, scale=st[("rs2", t)][:])
             banks = []
             for h in range(2):
                 bank = ps.tile([P, 512], F32, tag="tin", name="tbank")
@@ -521,14 +512,16 @@ def tile_mnelayer_pa_kernel(
                 nc.scalar.copy(out=of[:, 512 * h : 512 * h + 512], in_=st[("ubank", t)][h][:])
             nc.sync.dma_start(out=o0_v[:, t, :], in_=of[:])
 
-        def op_o(t):
+        def op_o(t, parts=1):
             if not okt(t) or t in TAIL_S:
                 return
             o = st[("o", t)]
-            nc.vector.scalar_tensor_tensor(
-                out=o[:], in0=o[:], scalar=st[("rs2", t)][:], in1=b_b[:], op0=ALU.mult, op1=ALU.add
-            )
-            nc.sync.dma_start(out=o0_v[:, t, :], in_=o[:])
+            for h in range(parts):
+                sl = slice(N // parts * h, N // parts * h + N // parts)
+                nc.vector.scalar_tensor_tensor(
+                    out=o[:, sl], in0=o[:, sl], scalar=st[("rs2", t)][:], in1=b_b[:, sl], op0=ALU.mult, op1=ALU.add
+                )
+                nc.sync.dma_start(out=o0_v[:, t, sl], in_=o[:, sl])
 
         load_x(0)
         load_x(1)
@@ -631,9 +624,11 @@ def tile_mnelayer_pa_kernel(
             qx(0)
             xT_pe(1)
             dd(1)
-            pe_sum(1)
+            pe_sum(1, 0)
+            pe_sum(1, 1)
             syn_prep(0)
-            cc(0)
+            cc(0, 0)
+            cc(0, 1)
             nm_s(1)
             zT_bank(0, 0)
             zT_bank(0, 1)
@@ -650,10 +645,17 @@ def tile_mnelayer_pa_kernel(
             qz(0)
             gw_prep(0)
             gw_prep(1)
-            bb(1)
-            syn_mx(0)
+            bb(1, 0)
+            bb(1, 1)
+            va_s(1)
+            syn_mx(0, 0)
+            syn_mx(0, 1)
 
         epi_box.append(ctx.enter_context(tc.tile_pool(name="epi", bufs=3)))
+        for i in range(4):
+            w = epi_box[0].tile([P, N + 8], F32, tag="w%d" % i, name="w", bufs=1)
+            nc.gpsimd.memset(w[:, N : N + 1], EPS**0.5 * 32)
+            w_box.append(w)
 
         gate_mx(0, 0)
         gate_mx(0, 1)
@@ -666,10 +668,12 @@ def tile_mnelayer_pa_kernel(
         gback(0)
         op_g(0)
         op_i(0)
-        syn_mx(1)
+        syn_mx(1, 0)
+        syn_mx(1, 1)
         powx(1)
         nr_s(1)
-        cc(1)
+        cc(1, 0)
+        cc(1, 1)
         op_j(0)
         zT_bank(1, 0)
         zT_bank(1, 1)
@@ -683,9 +687,8 @@ def tile_mnelayer_pa_kernel(
         zT_bank(1, 3)
 
         for tau in range(0, NT - 2):
+            m = tau // 2
             if tau % 2 == 0:
-                r = (tau + 2) // 2
-                r2 = r + 1
                 if tau - 2 < EARLY_POW:
                     pow_r(tau - 2)
                 np_g(tau - 1)
@@ -693,76 +696,74 @@ def tile_mnelayer_pa_kernel(
                 op_k(tau)
                 op_g(tau + 1)
                 tail_b(tau - 2)
-                e_bank(r, 2)
-                pe_sum(r2)
+                e_bank(m + 1, 2)
+                pe_sum(m + 2, 0)
+                pe_sum(m + 2, 1)
                 gback(tau + 1)
-                e_bank(r, 3)
-                if r >= 2 and RG1_ON_S:
-                    rg(r, 1, True)
-                v2(tau - 1)
+                e_bank(m + 1, 3)
                 if tau - 1 >= EARLY_POW:
                     pow_r(tau - 1)
                 op_o(tau - 2)
                 s1(tau)
                 op_i(tau + 1)
                 tail_c(tau - 2)
-                h_bank(r, 0)
-                gate_mx(r, 2)
-                h_bank(r, 1)
-                gate_mx(r, 3)
+                h_bank(m + 1, 0)
+                gate_mx(m + 1, 2)
+                h_bank(m + 1, 1)
+                gate_mx(m + 1, 3)
                 op_np(tau - 1)
                 s2(tau)
                 op_j(tau + 1)
-                if r == 1:
-                    rg(r, 0, False)
-                if r == 1 or not RG1_ON_S:
-                    rg(r, 1, False)
-                qz(r)
-                syn_mx(tau + 2)
-                nm_s(r2)
-                bb(r2)
+                if m == 0:
+                    rg(1, 0, False)
+                rg(m + 1, 1, False)
+                qz(m + 1)
+                syn_mx(tau + 2, 0)
+                syn_mx(tau + 2, 1)
+                nm_s(m + 2)
+                bb(m + 2, 0)
+                bb(m + 2, 1)
+                va_s(m + 2)
                 tail_a(tau - 1)
-                qx(r2)
+                qx(m + 2)
                 op_l(tau)
             else:
-                r1 = (tau + 1) // 2
-                r = r1 + 1
-                r2 = r1 + 2
                 if tau - 2 < EARLY_POW:
                     pow_r(tau - 2)
-                powx(r)
+                powx(m + 2)
                 np_g(tau - 1)
                 op_m(tau - 1)
                 op_k(tau)
                 op_g(tau + 1)
-                syn_mx(tau + 2)
-                h_bank(r1, 2)
-                v2(tau - 1)
+                syn_mx(tau + 2, 0)
+                syn_mx(tau + 2, 1)
+                h_bank(m + 1, 2)
                 if tau - 1 >= EARLY_POW:
                     pow_r(tau - 1)
-                gate_mx(r, 0)
-                h_bank(r1, 3)
-                gate_mx(r, 1)
+                gate_mx(m + 2, 0)
+                h_bank(m + 1, 3)
+                gate_mx(m + 2, 1)
                 gback(tau + 1)
                 tail_b(tau - 2)
                 op_o(tau - 2)
                 s1(tau)
                 op_i(tau + 1)
-                nr_s(r)
-                cc(r)
-                zT_bank(r, 0)
-                zT_bank(r, 1)
+                nr_s(m + 2)
+                cc(m + 2, 0)
+                cc(m + 2, 1)
+                zT_bank(m + 2, 0)
+                zT_bank(m + 2, 1)
                 op_np(tau - 1)
                 s2(tau)
                 op_j(tau + 1)
-                e_bank(r, 0)
-                e_bank(r, 1)
-                rg(r, 0, RG_ON_S and r >= 2)
+                e_bank(m + 2, 0)
+                e_bank(m + 2, 1)
+                rg(m + 2, 0, True)
                 tail_c(tau - 2)
-                xT_pe(r2)
-                dd(r2)
-                zT_bank(r, 2)
-                zT_bank(r, 3)
+                xT_pe(m + 3)
+                dd(m + 3)
+                zT_bank(m + 2, 2)
+                zT_bank(m + 2, 3)
                 tail_a(tau - 1)
                 op_l(tau)
 
@@ -770,7 +771,6 @@ def tile_mnelayer_pa_kernel(
         op_k(14)
         gback(15)
         op_g(15)
-        v2(13)
         pow_r(13)
         tail_b(12)
         s1(14)
@@ -784,7 +784,6 @@ def tile_mnelayer_pa_kernel(
         np_g(14)
         op_m(14)
         op_k(15)
-        v2(14)
         pow_r(14)
         tail_b(13)
         s1(15)
@@ -792,11 +791,9 @@ def tile_mnelayer_pa_kernel(
         s2(15)
         op_l(15)
 
-        np_g(15)
         op_m(15)
         op_np(15)
-        v2(15)
         pow_r(15)
         op_o(14)
         tail_c(13)
-        op_o(15)
+        op_o(15, 2)

@@ -23,10 +23,8 @@ FLOPS = 2 * 2 * B * N * N
 
 MANUAL = True
 RG_ON_S = True
-NP_BY_PARITY = (512, 768)
-SUMW = 128
+NP_BY_PARITY = (640, 896)
 RG1_ON_S = False
-EARLY_POW = 11
 TAIL_S = (11, 12, 13)
 
 
@@ -53,20 +51,23 @@ def tile_mnelayer_pa_kernel(
         make_identity(nc, idf[:])
         idb = res.tile([P, P], BF16, name="idb")
         make_identity(nc, idb[:])
-        mh = res.tile([P, 2], F32, name="mh")
+        mh = res.tile([P, 4], F32, name="mh")
         nc.gpsimd.memset(mh[:], -0.5)
         vec = res.tile([P, P], BF16, name="vec")
         nc.vector.memset(vec[:], 0.0)
         d0 = res.tile([P, 1], F32, name="d0")
         nc.vector.memset(d0[:], 0.0)
-        ones = res.tile([P, SUMW], BF16, name="ones")
-        nc.vector.memset(ones[:], 1.0)
         eps_t = res.tile([P, 1], F32, name="eps_t")
         nc.vector.memset(eps_t[:], EPS)
         d1 = res.tile([P, 1], F32, name="d1")
         nc.scalar.activation(out=d1[:], in_=d0[:], func=ACT.Sigmoid)
 
         x_t = [res.tile([P, 2 * N], BF16, name="x%d" % q) for q in range(NQ)]
+        XO = (32, 1120)
+        xg_t = [res.tile([P, 2176], BF16, name="xg%d" % i, align_bytes=64) for i in range(3)]
+        for i in range(3):
+            for o in (28, 1056):
+                nc.vector.memset(xg_t[i][:].rearrange("p (g c) -> p g c", g=2)[:, :, o : o + 4], 1.0)
         pv_t = [res.tile([P, 2 * N], BF16, name="pv%d" % q) for q in range(NQ)]
         g_b = res.tile([P, N], BF16, name="g_b")
         b_b = res.tile([P, N], BF16, name="b_b")
@@ -101,7 +102,7 @@ def tile_mnelayer_pa_kernel(
             xw = x_t[r][:].bitcast(F32)
             banks = []
             for g in range(2):
-                bank = ps.tile([P, 512], F32, tag="tin", name="xbank")
+                bank = ps.tile([P, 512], F32, tag="tin", bufs=4, name="xbank")
                 for u in range(2):
                     b = 2 * g + u
                     for ii in range(2):
@@ -116,36 +117,41 @@ def tile_mnelayer_pa_kernel(
         def dd(r):
             if not okr(r):
                 return
-            xg = pro.tile([P, 2048], BF16, tag="xg", name="xg", align_bytes=64, bufs=3)
+            xg = xg_t[r % 3]
             for g in range(2):
                 nc.scalar.copy(
-                    out=xg[:, 1024 * g : 1024 * g + 1024].bitcast(F32).rearrange("p (r u) -> p r u", u=2),
+                    out=xg[:, XO[g] : XO[g] + 1024].bitcast(F32).rearrange("p (r u) -> p r u", u=2),
                     in_=st[("xbank", r)][g][:].rearrange("p (u r) -> p r u", u=2),
                 )
-            st[("xg", r)] = [xg[:, 1024 * g : 1024 * g + 1024] for g in range(2)]
-            st[("xgt", r)] = xg
+            st[("xg", r)] = xg
 
         def qx(r):
             if not okr(r):
                 return
             xc = pro.tile([P, 512], U32, tag="xc", name="xc", align_bytes=64)
             xs = pro.tile([P, 512], U8, tag="xs", name="xs", align_bytes=64)
-            nc.vector.quantize_mx(out=xc[:].bitcast(FP8X4), scales=xs[:], in_=st[("xgt", r)][:])
+            for g in range(2):
+                nc.vector.quantize_mx(
+                    out=xc[:, 256 * g : 256 * g + 256].bitcast(FP8X4),
+                    scales=xs[:, 256 * g : 256 * g + 256],
+                    in_=st[("xg", r)][:, XO[g] : XO[g] + 1024],
+                )
             st[("xc", r)] = (xc, xs)
 
         def pe_sum(r, ii):
             if not okr(r):
                 return
             if ii == 0:
-                st[("sbank", r)] = ps.tile([P, 2 * SUMW], F32, tag="tin", name="sbank")
+                st[("sbank", r)] = ps.tile([P, 512], F32, tag="tin", bufs=4, name="sbank")
             bank = st[("sbank", r)]
             for g in range(2):
-                xv = st[("xg", r)][g].rearrange("p (r t) -> p r t", t=4)
                 for t in range(4):
+                    o = XO[g] + 512 * ii + t
+                    m = o - 4 * (1 - ii)
                     nc.tensor.matmul(
-                        out=bank[:, SUMW * ii : SUMW * ii + SUMW],
-                        lhsT=xv[:, 128 * ii : 128 * ii + 128, t],
-                        rhs=ones[:],
+                        out=bank[:, 256 * ii : 256 * ii + 129],
+                        lhsT=st[("xg", r)][:, o : o + 509 : 4],
+                        rhs=st[("xg", r)][:, m : m + 513 : 4],
                         start=(g == 0 and t == 0),
                         stop=(g == 1 and t == 3),
                     )
@@ -154,39 +160,66 @@ def tile_mnelayer_pa_kernel(
             if not okr(r):
                 return
             nm = sml.tile([P, 2], F32, tag="nm", name="nm", bufs=6)
-            nc.scalar.mul(
-                out=nm[:], in_=st[("sbank", r)][:].rearrange("p (i c) -> p i c", c=SUMW)[:, :, 0], mul=-1.0 / N
-            )
+            nc.scalar.mul(out=nm[:], in_=st[("sbank", r)][:, 0:385:384], mul=-1.0 / N)
             st[("nm", r)] = nm
 
-        def bb(r, ii):
+        def m2_s(r):
             if not okr(r):
                 return
-            nm = st[("nm", r)]
-            if ii == 0:
-                st[("sq", r)] = sml.tile([P, 2], F32, tag="sq", name="sq")
-            junk = pro.tile([P, N + 2], BF16, tag="junk", name="junk")
-            nc.scalar.activation(
-                out=junk[:, 0:N],
-                in_=x_t[r][:, N * ii : N * ii + N],
-                func=ACT.Square,
-                bias=nm[:, ii : ii + 1],
-                accum_out=st[("sq", r)][:, ii : ii + 1],
+            m2 = sml.tile([P, 2], F32, tag="m2", name="m2")
+            nc.scalar.activation(out=m2[:], in_=st[("nm", r)][:], func=ACT.Square)
+            st[("m2", r)] = m2
+
+        def dg(r):
+            if not okr(r):
+                return
+            sq = sml.tile([P, 2], F32, tag="sq", name="sq")
+            for ii in range(2):
+                jd = pro.tile([P, P], F32, tag="jd", name="jd")
+                nc.vector.scalar_tensor_tensor(
+                    out=jd[:],
+                    in0=st[("sbank", r)][:, 255 * ii + 1 : 255 * ii + 129],
+                    scalar=1.0,
+                    in1=idf[:],
+                    op0=ALU.mult,
+                    op1=ALU.mult,
+                    accum_out=sq[:, ii : ii + 1],
+                )
+            st[("sq", r)] = sq
+
+        def va_b(r):
+            if not okr(r):
+                return
+            vb = sml.tile([P, 2], F32, tag="vb", name="vb")
+            nc.vector.scalar_tensor_tensor(
+                out=vb[:], in0=st[("sq", r)][:], scalar=1.0 / N, in1=st[("m2", r)][:], op0=ALU.mult, op1=ALU.subtract
+            )
+            st[("vb", r)] = vb
+
+        def pw_tile(m):
+            if ("pw", m) not in st:
+                st[("pw", m)] = sml.tile([P, 4], F32, tag="pw", name="pw")
+            return st[("pw", m)]
+
+        def va_c(r):
+            if not okr(r):
+                return
+            nc.vector.tensor_scalar(
+                out=pw_tile(r - 2)[:, 0:2], in0=st[("vb", r)][:], scalar1=0.0, scalar2=EPS, op0=ALU.max, op1=ALU.add
             )
 
-        def va_s(r):
-            if not okr(r):
+        def pows(m):
+            x, r = okr(m + 2), 1 <= m <= 5
+            if not (x or r):
                 return
-            va = sml.tile([P, 2], F32, tag="va", name="va")
-            nc.scalar.activation(out=va[:], in_=st[("sq", r)][:], func=ACT.Identity, scale=1.0 / N, bias=eps_t[:])
-            st[("va", r)] = va
-
-        def powx(r):
-            if not okr(r):
-                return
-            rs = sml.tile([P, 2], F32, tag="rs", name="rs")
-            nc.gpsimd.tensor_tensor(out=rs[:], in0=st[("va", r)][:], in1=mh[:], op=ALU.pow)
-            st[("rs1", r)] = rs
+            sl = slice(0 if x else 2, 4 if r else 2)
+            rs = sml.tile([P, 4], F32, tag="rs", name="rs")
+            nc.gpsimd.tensor_tensor(out=rs[:, sl], in0=st[("pw", m)][:, sl], in1=mh[:, sl], op=ALU.pow)
+            if x:
+                st[("rs1", m + 2)] = rs
+            if r:
+                st[("rs2", 2 * m - 2)] = rs[:, 2:3]
+                st[("rs2", 2 * m - 1)] = rs[:, 3:4]
 
         def nr_s(r):
             if not okr(r):
@@ -221,7 +254,7 @@ def tile_mnelayer_pa_kernel(
             if not okr(r):
                 return
             z = st[("z", r)]
-            bank = ps.tile([P, 512], F32, tag="tin", name="zbank")
+            bank = ps.tile([P, 512], F32, tag="tin", bufs=4, name="zbank")
             for jj in range(2):
                 j = 2 * b + jj
                 for ii in range(2):
@@ -275,7 +308,7 @@ def tile_mnelayer_pa_kernel(
             if not okr(r):
                 return
             xc, xs = st[("xc", r)]
-            bank = ps.tile([P, 512], F32, tag="gt", name="gtbank")
+            bank = ps.tile([P, 512], F32, tag="tin", bufs=4, name="gtbank")
             for jj in range(2):
                 j = 2 * b + jj
                 for g in range(2):
@@ -427,19 +460,22 @@ def tile_mnelayer_pa_kernel(
         def op_m(t):
             if not okt(t):
                 return
-            sq2 = sml.tile([P, 1], F32, tag="sq2", name="sq2")
+            if t < 10:
+                sq2 = pw_tile(t // 2 + 1)[:, 2 + t % 2 : 3 + t % 2]
+            else:
+                st[("sq2", t)] = sml.tile([P, 1], F32, tag="sq2", name="sq2")
+                sq2 = st[("sq2", t)][:]
             junk = pro.tile([P, N + 2], BF16, tag="junk", name="junk")
             nc.scalar.activation(
-                out=junk[:, 0 : N + 1], in_=st[("w", t)][:, 0 : N + 1], func=ACT.Square, scale=1.0 / 32, accum_out=sq2[:]
+                out=junk[:, 0 : N + 1], in_=st[("w", t)][:, 0 : N + 1], func=ACT.Square, scale=1.0 / 32, accum_out=sq2
             )
-            st[("sq2", t)] = sq2
 
         def pow_r(t):
             if not okt(t):
                 return
             rs2 = sml.tile([P, 1], F32, tag="rs2", name="rs2")
             nc.gpsimd.tensor_tensor(out=rs2[:], in0=st[("sq2", t)][:], in1=mh[:, 0:1], op=ALU.pow)
-            st[("rs2", t)] = rs2
+            st[("rs2", t)] = rs2[:]
 
         def np_alloc(t):
             if ("o", t) not in st:
@@ -467,10 +503,10 @@ def tile_mnelayer_pa_kernel(
             if t not in TAIL_S:
                 return
             t1 = epi_box[0].tile([P, N], F32, tag="tl", name="t1", bufs=5)
-            nc.scalar.activation(out=t1[:], in_=st[("w", t)][:, 0:N], func=ACT.Identity, scale=st[("rs2", t)][:])
+            nc.scalar.activation(out=t1[:], in_=st[("w", t)][:, 0:N], func=ACT.Identity, scale=st[("rs2", t)])
             banks = []
             for h in range(2):
-                bank = ps.tile([P, 512], F32, tag="tin", name="tbank")
+                bank = ps.tile([P, 512], F32, tag="tin", bufs=4, name="tbank")
                 for jj in range(4):
                     j = 4 * h + jj
                     nc.tensor.transpose(
@@ -495,7 +531,7 @@ def tile_mnelayer_pa_kernel(
                     )
             banks = []
             for h in range(2):
-                bank = ps.tile([P, 512], F32, tag="gt", name="ubank")
+                bank = ps.tile([P, 512], F32, tag="tin", bufs=4, name="ubank")
                 for jj in range(4):
                     j = 4 * h + jj
                     nc.tensor.transpose(
@@ -519,7 +555,7 @@ def tile_mnelayer_pa_kernel(
             for h in range(parts):
                 sl = slice(N // parts * h, N // parts * h + N // parts)
                 nc.vector.scalar_tensor_tensor(
-                    out=o[:, sl], in0=o[:, sl], scalar=st[("rs2", t)][:], in1=b_b[:, sl], op0=ALU.mult, op1=ALU.add
+                    out=o[:, sl], in0=o[:, sl], scalar=st[("rs2", t)], in1=b_b[:, sl], op0=ALU.mult, op1=ALU.add
                 )
                 nc.sync.dma_start(out=o0_v[:, t, sl], in_=o[:, sl])
 
@@ -573,7 +609,7 @@ def tile_mnelayer_pa_kernel(
                     grp = wt.tile([P, 2048], BF16, tag="wgrp", name="ggrp", bufs=6, align_bytes=64)
                     grw = grp[:].bitcast(F32)
                     for jq in range(2):
-                        bank = ps.tile([P, 512], F32, tag="tin", name="gbank")
+                        bank = ps.tile([P, 512], F32, tag="tin", bufs=4, name="gbank")
                         for u in range(2):
                             b = 2 * g + u
                             for j2 in range(2):
@@ -611,14 +647,16 @@ def tile_mnelayer_pa_kernel(
             nc.vector.tensor_scalar(out=va0[:], in0=mvv[:, :, 1], scalar1=EPS, scalar2=None, op0=ALU.add)
             st[("nm", 0)] = nm0
             st[("va", 0)] = va0
-            powx(0)
+            rs0 = sml.tile([P, 4], F32, tag="rs", name="rs")
+            nc.gpsimd.tensor_tensor(out=rs0[:, 0:2], in0=va0[:], in1=mh[:, 0:2], op=ALU.pow)
+            st[("rs1", 0)] = rs0
             nr0 = sml.tile([P, 2], F32, tag="nr", name="nr")
-            nc.vector.tensor_tensor(out=nr0[:], in0=nm0[:], in1=st[("rs1", 0)][:], op=ALU.mult)
-            st[("rs", 0)] = (st[("rs1", 0)], nr0)
+            nc.vector.tensor_tensor(out=nr0[:], in0=nm0[:], in1=rs0[:, 0:2], op=ALU.mult)
+            st[("rs", 0)] = (rs0, nr0)
 
             xT_pe(0)
             dd(0)
-            vbank = ps.tile([P, P], BF16, tag="gt", name="vbank")
+            vbank = ps.tile([P, P], BF16, tag="tin", bufs=4, name="vbank")
             nc.tensor.transpose(out=vbank[:], in_=vec[:], identity=idb[:])
             nc.vector.tensor_copy(out=vT[:, 0:40], in_=vbank[:, 0:40])
             qx(0)
@@ -626,10 +664,11 @@ def tile_mnelayer_pa_kernel(
             dd(1)
             pe_sum(1, 0)
             pe_sum(1, 1)
+            cc(0, 0, True)
+            cc(0, 1, True)
             syn_prep(0)
-            cc(0, 0)
-            cc(0, 1)
             nm_s(1)
+            m2_s(1)
             zT_bank(0, 0)
             zT_bank(0, 1)
             e_bank(0, 0)
@@ -638,16 +677,20 @@ def tile_mnelayer_pa_kernel(
             zT_bank(0, 3)
             e_bank(0, 2)
             e_bank(0, 3)
+            dg(1)
+            va_b(1)
             syn_prep(1)
+            va_c(1)
             qx(1)
             rg(0, 0, False)
             rg(0, 1, False)
             qz(0)
+            pows(-1)
             gw_prep(0)
             gw_prep(1)
-            bb(1, 0)
-            bb(1, 1)
-            va_s(1)
+            nr_s(1)
+            cc(1, 0)
+            cc(1, 1)
             syn_mx(0, 0)
             syn_mx(0, 1)
 
@@ -659,26 +702,20 @@ def tile_mnelayer_pa_kernel(
 
         gate_mx(0, 0)
         gate_mx(0, 1)
-        h_bank(0, 0)
         gate_mx(0, 2)
-        h_bank(0, 1)
+        h_bank(0, 0)
         gate_mx(0, 3)
+        h_bank(0, 1)
         h_bank(0, 2)
         h_bank(0, 3)
-        gback(0)
         op_g(0)
         op_i(0)
         syn_mx(1, 0)
         syn_mx(1, 1)
-        powx(1)
-        nr_s(1)
-        cc(1, 0)
-        cc(1, 1)
+        gback(0)
         op_j(0)
         zT_bank(1, 0)
         zT_bank(1, 1)
-        gate_mx(1, 0)
-        gate_mx(1, 1)
         e_bank(1, 0)
         e_bank(1, 1)
         xT_pe(2)
@@ -689,84 +726,80 @@ def tile_mnelayer_pa_kernel(
         for tau in range(0, NT - 2):
             m = tau // 2
             if tau % 2 == 0:
-                if tau - 2 < EARLY_POW:
-                    pow_r(tau - 2)
                 np_g(tau - 1)
-                op_m(tau - 1)
+                e_bank(m + 1, 2)
+                e_bank(m + 1, 3)
                 op_k(tau)
                 op_g(tau + 1)
+                gback(tau + 1)
                 tail_b(tau - 2)
-                e_bank(m + 1, 2)
                 pe_sum(m + 2, 0)
                 pe_sum(m + 2, 1)
-                gback(tau + 1)
-                e_bank(m + 1, 3)
-                if tau - 1 >= EARLY_POW:
+                op_m(tau - 1)
+                if tau - 1 >= 10:
                     pow_r(tau - 1)
-                op_o(tau - 2)
+                rg(m + 1, 0, m > 0)
+                rg(m + 1, 1, m > 0)
+                nm_s(m + 2)
+                op_o(tau - 3)
                 s1(tau)
                 op_i(tau + 1)
                 tail_c(tau - 2)
+                gate_mx(m + 1, 0)
+                gate_mx(m + 1, 1)
                 h_bank(m + 1, 0)
+                m2_s(m + 2)
                 gate_mx(m + 1, 2)
                 h_bank(m + 1, 1)
                 gate_mx(m + 1, 3)
+                h_bank(m + 1, 2)
+                h_bank(m + 1, 3)
                 op_np(tau - 1)
                 s2(tau)
                 op_j(tau + 1)
-                if m == 0:
-                    rg(1, 0, False)
-                rg(m + 1, 1, False)
                 qz(m + 1)
                 syn_mx(tau + 2, 0)
                 syn_mx(tau + 2, 1)
-                nm_s(m + 2)
-                bb(m + 2, 0)
-                bb(m + 2, 1)
-                va_s(m + 2)
-                tail_a(tau - 1)
-                qx(m + 2)
+                dg(m + 2)
                 op_l(tau)
+                va_b(m + 2)
+                qx(m + 2)
+                va_c(m + 2)
+                tail_a(tau - 1)
             else:
-                if tau - 2 < EARLY_POW:
-                    pow_r(tau - 2)
-                powx(m + 2)
+                pows(m)
                 np_g(tau - 1)
-                op_m(tau - 1)
                 op_k(tau)
                 op_g(tau + 1)
                 syn_mx(tau + 2, 0)
                 syn_mx(tau + 2, 1)
-                h_bank(m + 1, 2)
-                if tau - 1 >= EARLY_POW:
-                    pow_r(tau - 1)
-                gate_mx(m + 2, 0)
-                h_bank(m + 1, 3)
-                gate_mx(m + 2, 1)
                 gback(tau + 1)
-                tail_b(tau - 2)
-                op_o(tau - 2)
-                s1(tau)
-                op_i(tau + 1)
                 nr_s(m + 2)
                 cc(m + 2, 0)
                 cc(m + 2, 1)
+                op_m(tau - 1)
+                if tau - 1 >= 10:
+                    pow_r(tau - 1)
+                tail_b(tau - 2)
+                op_o(tau - 3)
+                s1(tau)
+                op_i(tau + 1)
                 zT_bank(m + 2, 0)
                 zT_bank(m + 2, 1)
                 op_np(tau - 1)
                 s2(tau)
                 op_j(tau + 1)
+                xT_pe(m + 3)
                 e_bank(m + 2, 0)
                 e_bank(m + 2, 1)
-                rg(m + 2, 0, True)
                 tail_c(tau - 2)
-                xT_pe(m + 3)
                 dd(m + 3)
                 zT_bank(m + 2, 2)
                 zT_bank(m + 2, 3)
-                tail_a(tau - 1)
                 op_l(tau)
+                tail_a(tau - 1)
 
+        op_o(11)
         op_m(13)
         op_k(14)
         gback(15)

@@ -221,6 +221,12 @@ def tile_mnelayer_pa_kernel(
                 st[("rs2", 2 * m - 2)] = rs[:, 2:3]
                 st[("rs2", 2 * m - 1)] = rs[:, 3:4]
 
+        def nr_v(r):
+            rs = st[("rs1", r)]
+            nr = sml.tile([P, 2], F32, tag="nr", name="nr")
+            nc.vector.tensor_tensor(out=nr[:], in0=st[("nm", r)][:], in1=rs[:, 0:2], op=ALU.mult)
+            st[("rs", r)] = (rs, nr)
+
         def nr_s(r):
             if not okr(r):
                 return
@@ -483,7 +489,7 @@ def tile_mnelayer_pa_kernel(
             return st[("o", t)]
 
         def np_split(t):
-            return 0 if t == NT - 1 else NP_BY_PARITY[t % 2]
+            return {14: 384, 15: 0}.get(t, NP_BY_PARITY[t % 2])
 
         def np_g(t):
             if not okt(t) or t in TAIL_S:
@@ -679,18 +685,26 @@ def tile_mnelayer_pa_kernel(
             e_bank(0, 3)
             dg(1)
             va_b(1)
-            syn_prep(1)
             va_c(1)
+            pows(-1)
             qx(1)
+            nr_v(1)
+            syn_prep(1)
             rg(0, 0, False)
             rg(0, 1, False)
             qz(0)
-            pows(-1)
             gw_prep(0)
-            gw_prep(1)
-            nr_s(1)
             cc(1, 0)
             cc(1, 1)
+            gw_prep(1)
+            zT_bank(1, 0)
+            zT_bank(1, 1)
+            e_bank(1, 0)
+            zT_bank(1, 2)
+            e_bank(1, 1)
+            zT_bank(1, 3)
+            e_bank(1, 2)
+            e_bank(1, 3)
             syn_mx(0, 0)
             syn_mx(0, 1)
 
@@ -709,26 +723,23 @@ def tile_mnelayer_pa_kernel(
         h_bank(0, 2)
         h_bank(0, 3)
         op_g(0)
+        rg(1, 0, False)
         op_i(0)
         syn_mx(1, 0)
         syn_mx(1, 1)
         gback(0)
+        rg(1, 1, False)
         op_j(0)
-        zT_bank(1, 0)
-        zT_bank(1, 1)
-        e_bank(1, 0)
-        e_bank(1, 1)
         xT_pe(2)
         dd(2)
-        zT_bank(1, 2)
-        zT_bank(1, 3)
 
         for tau in range(0, NT - 2):
             m = tau // 2
             if tau % 2 == 0:
                 np_g(tau - 1)
-                e_bank(m + 1, 2)
-                e_bank(m + 1, 3)
+                if m > 0:
+                    e_bank(m + 1, 2)
+                    e_bank(m + 1, 3)
                 op_k(tau)
                 op_g(tau + 1)
                 gback(tau + 1)
@@ -738,8 +749,9 @@ def tile_mnelayer_pa_kernel(
                 op_m(tau - 1)
                 if tau - 1 >= 10:
                     pow_r(tau - 1)
-                rg(m + 1, 0, m > 0)
-                rg(m + 1, 1, m > 0)
+                if m > 0:
+                    rg(m + 1, 0, True)
+                    rg(m + 1, 1, True)
                 nm_s(m + 2)
                 op_o(tau - 3)
                 s1(tau)
@@ -757,12 +769,12 @@ def tile_mnelayer_pa_kernel(
                 op_np(tau - 1)
                 s2(tau)
                 op_j(tau + 1)
-                qz(m + 1)
-                syn_mx(tau + 2, 0)
-                syn_mx(tau + 2, 1)
                 dg(m + 2)
                 op_l(tau)
                 va_b(m + 2)
+                qz(m + 1)
+                syn_mx(tau + 2, 0)
+                syn_mx(tau + 2, 1)
                 qx(m + 2)
                 va_c(m + 2)
                 tail_a(tau - 1)
@@ -771,15 +783,17 @@ def tile_mnelayer_pa_kernel(
                 np_g(tau - 1)
                 op_k(tau)
                 op_g(tau + 1)
+                op_m(tau - 1)
+                if tau - 1 >= 10:
+                    pow_r(tau - 1)
                 syn_mx(tau + 2, 0)
                 syn_mx(tau + 2, 1)
                 gback(tau + 1)
                 nr_s(m + 2)
                 cc(m + 2, 0)
                 cc(m + 2, 1)
-                op_m(tau - 1)
-                if tau - 1 >= 10:
-                    pow_r(tau - 1)
+                xT_pe(m + 3)
+                dd(m + 3)
                 tail_b(tau - 2)
                 op_o(tau - 3)
                 s1(tau)
@@ -789,17 +803,14 @@ def tile_mnelayer_pa_kernel(
                 op_np(tau - 1)
                 s2(tau)
                 op_j(tau + 1)
-                xT_pe(m + 3)
                 e_bank(m + 2, 0)
                 e_bank(m + 2, 1)
                 tail_c(tau - 2)
-                dd(m + 3)
                 zT_bank(m + 2, 2)
                 zT_bank(m + 2, 3)
                 op_l(tau)
                 tail_a(tau - 1)
 
-        op_o(11)
         op_m(13)
         op_k(14)
         gback(15)
@@ -825,8 +836,8 @@ def tile_mnelayer_pa_kernel(
         op_l(15)
 
         op_m(15)
+        op_o(14)
         op_np(15)
         pow_r(15)
-        op_o(14)
         tail_c(13)
         op_o(15, 2)

from contextlib import ExitStack

import concourse.mybir as mybir
from concourse.masks import make_identity

F32 = mybir.dt.float32
BF16 = mybir.dt.bfloat16
U32 = mybir.dt.uint32
U8 = mybir.dt.uint8
FP8X4 = mybir.dt.float8_e4m3fn_x4
ALU = mybir.AluOpType
ACT = mybir.ActivationFunctionType

P = 128
B = 2048
N = 1024
NT = 16
NQ = 8
EPS = 1e-5
DECAY = 0.9
SLOPE = 0.01
FLOPS = 2 * 2 * B * N * N

MANUAL = True
RG_ON_S = True
NP_BY_PARITY = (640, 896)
RG1_ON_S = False
TAIL_S = (11, 12, 13)


def tile_mnelayer_pa_kernel(
    tc, inputs, prev_potential, syn_weights, gate_W, gate_b, pre_gamma, pre_beta, ln_gamma, ln_beta, out_0, out_1
):
    nc = tc.nc
    x_v = inputs.rearrange("(p i) k -> p i k", i=NT)
    pv_v = prev_potential.rearrange("(p i) k -> p i k", i=NT)
    o0_v = out_0.rearrange("(p i) n -> p i n", i=NT)
    o1_v = out_1.rearrange("(p i) n -> p i n", i=NT)
    syn_v = syn_weights.rearrange("(c t p) n -> c p t n", t=4, p=P)
    gw_v = gate_W.rearrange("(h j m) k -> h m j k", j=4, m=P)

    with ExitStack() as ctx:
        if MANUAL:
            ctx.enter_context(tc.manual_schedule())
        res = ctx.enter_context(tc.tile_pool(name="res", bufs=1))
        pro = ctx.enter_context(tc.tile_pool(name="pro", bufs=2))
        sml = ctx.enter_context(tc.tile_pool(name="sml", bufs=4))
        ps = ctx.enter_context(tc.psum_pool(name="ps", bufs=2))

        idf = res.tile([P, P], F32, name="idf")
        make_identity(nc, idf[:])
        idb = res.tile([P, P], BF16, name="idb")
        make_identity(nc, idb[:])
        mh = res.tile([P, 4], F32, name="mh")
        nc.gpsimd.memset(mh[:], -0.5)
        vec = res.tile([P, P], BF16, name="vec")
        nc.vector.memset(vec[:], 0.0)
        d0 = res.tile([P, 1], F32, name="d0")
        nc.vector.memset(d0[:], 0.0)
        eps_t = res.tile([P, 1], F32, name="eps_t")
        nc.vector.memset(eps_t[:], EPS)
        d1 = res.tile([P, 1], F32, name="d1")
        nc.scalar.activation(out=d1[:], in_=d0[:], func=ACT.Sigmoid)

        x_t = [res.tile([P, 2 * N], BF16, name="x%d" % q) for q in range(NQ)]
        XO = (32, 1120)
        xg_t = [res.tile([P, 2176], BF16, name="xg%d" % i, align_bytes=64) for i in range(3)]
        for i in range(3):
            for o in (28, 1056):
                nc.vector.memset(xg_t[i][:].rearrange("p (g c) -> p g c", g=2)[:, :, o : o + 4], 1.0)
        pv_t = [res.tile([P, 2 * N], BF16, name="pv%d" % q) for q in range(NQ)]
        g_b = res.tile([P, N], BF16, name="g_b")
        b_b = res.tile([P, N], BF16, name="b_b")
        sc = res.tile([P, 2 * N], U32, name="sc", align_bytes=64)
        ss = res.tile([P, 2 * N], U8, name="ss", align_bytes=64)
        gwc = res.tile([P, 2 * N], U32, name="gwc", align_bytes=64)
        gws = res.tile([P, 2 * N], U8, name="gws", align_bytes=64)
        vT = res.tile([P, 40], F32, name="vT")

        def load_x(q):
            nc.sync.dma_start(out=x_t[q][:].rearrange("p (i k) -> p i k", i=2), in_=x_v[:, 2 * q : 2 * q + 2, :])

        def load_pv(q):
            nc.sync.dma_start(out=pv_t[q][:].rearrange("p (i k) -> p i k", i=2), in_=pv_v[:, 2 * q : 2 * q + 2, :])

        st = {}
        epi_box = []
        w_box = []

        def okr(r):
            return 0 <= r < NQ

        def okt(t):
            return 0 <= t < NT

        def x_of(t):
            return x_t[t // 2][:, N * (t % 2) : N * (t % 2) + N]

        def xT_pe(r):
            if not okr(r):
                return
            xw = x_t[r][:].bitcast(F32)
            banks = []
            for g in range(2):
                bank = ps.tile([P, 512], F32, tag="tin", bufs=4, name="xbank")
                for u in range(2):
                    b = 2 * g + u
                    for ii in range(2):
                        nc.tensor.transpose(
                            out=bank[:, 256 * u + 128 * ii : 256 * u + 128 * ii + 128],
                            in_=xw[:, 512 * ii + 128 * b : 512 * ii + 128 * b + 128],
                            identity=idf[:],
                        )
                banks.append(bank)
            st[("xbank", r)] = banks

        def dd(r):
            if not okr(r):
                return
            xg = xg_t[r % 3]
            for g in range(2):
                nc.scalar.copy(
                    out=xg[:, XO[g] : XO[g] + 1024].bitcast(F32).rearrange("p (r u) -> p r u", u=2),
                    in_=st[("xbank", r)][g][:].rearrange("p (u r) -> p r u", u=2),
                )
            st[("xg", r)] = xg

        def qx(r):
            if not okr(r):
                return
            xc = pro.tile([P, 512], U32, tag="xc", name="xc", align_bytes=64)
            xs = pro.tile([P, 512], U8, tag="xs", name="xs", align_bytes=64)
            for g in range(2):
                nc.vector.quantize_mx(
                    out=xc[:, 256 * g : 256 * g + 256].bitcast(FP8X4),
                    scales=xs[:, 256 * g : 256 * g + 256],
                    in_=st[("xg", r)][:, XO[g] : XO[g] + 1024],
                )
            st[("xc", r)] = (xc, xs)

        def pe_sum(r, ii):
            if not okr(r):
                return
            if ii == 0:
                st[("sbank", r)] = ps.tile([P, 512], F32, tag="tin", bufs=4, name="sbank")
            bank = st[("sbank", r)]
            for g in range(2):
                for t in range(4):
                    o = XO[g] + 512 * ii + t
                    m = o - 4 * (1 - ii)
                    nc.tensor.matmul(
                        out=bank[:, 256 * ii : 256 * ii + 129],
                        lhsT=st[("xg", r)][:, o : o + 509 : 4],
                        rhs=st[("xg", r)][:, m : m + 513 : 4],
                        start=(g == 0 and t == 0),
                        stop=(g == 1 and t == 3),
                    )

        def nm_s(r):
            if not okr(r):
                return
            nm = sml.tile([P, 2], F32, tag="nm", name="nm", bufs=6)
            nc.scalar.mul(out=nm[:], in_=st[("sbank", r)][:, 0:385:384], mul=-1.0 / N)
            st[("nm", r)] = nm

        def m2_s(r):
            if not okr(r):
                return
            m2 = sml.tile([P, 2], F32, tag="m2", name="m2")
            nc.scalar.activation(out=m2[:], in_=st[("nm", r)][:], func=ACT.Square)
            st[("m2", r)] = m2

        def dg(r):
            if not okr(r):
                return
            sq = sml.tile([P, 2], F32, tag="sq", name="sq")
            for ii in range(2):
                jd = pro.tile([P, P], F32, tag="jd", name="jd")
                nc.vector.scalar_tensor_tensor(
                    out=jd[:],
                    in0=st[("sbank", r)][:, 255 * ii + 1 : 255 * ii + 129],
                    scalar=1.0,
                    in1=idf[:],
                    op0=ALU.mult,
                    op1=ALU.mult,
                    accum_out=sq[:, ii : ii + 1],
                )
            st[("sq", r)] = sq

        def va_b(r):
            if not okr(r):
                return
            vb = sml.tile([P, 2], F32, tag="vb", name="vb")
            nc.vector.scalar_tensor_tensor(
                out=vb[:], in0=st[("sq", r)][:], scalar=1.0 / N, in1=st[("m2", r)][:], op0=ALU.mult, op1=ALU.subtract
            )
            st[("vb", r)] = vb

        def pw_tile(m):
            if ("pw", m) not in st:
                st[("pw", m)] = sml.tile([P, 4], F32, tag="pw", name="pw")
            return st[("pw", m)]

        def va_c(r):
            if not okr(r):
                return
            nc.vector.tensor_scalar(
                out=pw_tile(r - 2)[:, 0:2], in0=st[("vb", r)][:], scalar1=0.0, scalar2=EPS, op0=ALU.max, op1=ALU.add
            )

        def pows(m):
            x, r = okr(m + 2), 1 <= m <= 5
            if not (x or r):
                return
            sl = slice(0 if x else 2, 4 if r else 2)
            rs = sml.tile([P, 4], F32, tag="rs", name="rs")
            nc.gpsimd.tensor_tensor(out=rs[:, sl], in0=st[("pw", m)][:, sl], in1=mh[:, sl], op=ALU.pow)
            if x:
                st[("rs1", m + 2)] = rs
            if r:
                st[("rs2", 2 * m - 2)] = rs[:, 2:3]
                st[("rs2", 2 * m - 1)] = rs[:, 3:4]

        def nr_v(r):
            rs = st[("rs1", r)]
            nr = sml.tile([P, 2], F32, tag="nr", name="nr")
            nc.vector.tensor_tensor(out=nr[:], in0=st[("nm", r)][:], in1=rs[:, 0:2], op=ALU.mult)
            st[("rs", r)] = (rs, nr)

        def nr_s(r):
            if not okr(r):
                return
            rs = st[("rs1", r)]
            nm = st[("nm", r)]
            nr = sml.tile([P, 2], F32, tag="nr", name="nr")
            for ii in range(2):
                nc.scalar.activation(
                    out=nr[:, ii : ii + 1], in_=nm[:, ii : ii + 1], func=ACT.Identity, scale=rs[:, ii : ii + 1]
                )
            st[("rs", r)] = (rs, nr)

        def cc(r, ii, on_v=False):
            if not okr(r):
                return
            if ii == 0:
                st[("z", r)] = pro.tile([P, 2 * N], F32, tag="z", name="z")
            z = st[("z", r)][:, N * ii : N * ii + N]
            x = x_t[r][:, N * ii : N * ii + N]
            rs, nr = st[("rs", r)]
            if on_v:
                nc.vector.tensor_scalar(
                    out=z, in0=x, scalar1=rs[:, ii : ii + 1], scalar2=nr[:, ii : ii + 1], op0=ALU.mult, op1=ALU.add
                )
            else:
                nc.scalar.activation(
                    out=z, in_=x, func=ACT.Identity, scale=rs[:, ii : ii + 1], bias=nr[:, ii : ii + 1]
                )

        def zT_bank(r, b):
            if not okr(r):
                return
            z = st[("z", r)]
            bank = ps.tile([P, 512], F32, tag="tin", bufs=4, name="zbank")
            for jj in range(2):
                j = 2 * b + jj
                for ii in range(2):
                    nc.tensor.transpose(
                        out=bank[:, 256 * jj + 128 * ii : 256 * jj + 128 * ii + 128],
                        in_=z[:, N * ii + 128 * j : N * ii + 128 * j + 128],
                        identity=idf[:],
                    )
            st[("zbank", r, b)] = bank

        def e_bank(r, b):
            if not okr(r):
                return
            c = b // 2
            if b % 2 == 0:
                st[("zp", r, c)] = pro.tile([P, 1024], BF16, tag="zp", name="zp")
            zp = st[("zp", r, c)]
            bank = st[("zbank", r, b)]
            for jj in range(2):
                j = 2 * b + jj
                t = j % 4
                nc.scalar.activation(
                    out=zp[:, 256 * t : 256 * t + 256],
                    in_=bank[:, 256 * jj : 256 * jj + 256],
                    func=ACT.Identity,
                    scale=vT[:, 8 + j : 9 + j],
                    bias=vT[:, 16 + j : 17 + j],
                )

        def rg(r, c, on_s):
            if not okr(r):
                return
            if c == 0:
                st[("zg", r)] = pro.tile([P, 2048], BF16, tag="zg", name="zg", align_bytes=64)
            src = st[("zp", r, c)][:].rearrange("p (t a i) -> p a t i", t=4, i=4)
            dst = st[("zg", r)][:, 1024 * c : 1024 * c + 1024].rearrange("p (a i t) -> p a t i", i=4, t=4)
            if on_s:
                nc.scalar.copy(out=dst, in_=src)
            else:
                nc.vector.tensor_copy(out=dst, in_=src)

        def qz(r):
            if not okr(r):
                return
            zc = pro.tile([P, 512], U32, tag="zc", name="zc", align_bytes=64)
            zs = pro.tile([P, 512], U8, tag="zs", name="zs", align_bytes=64)
            nc.vector.quantize_mx(out=zc[:].bitcast(FP8X4), scales=zs[:], in_=st[("zg", r)][:])
            st[("zc", r)] = (zc, zs)

        def gate_mx(r, b):
            if not okr(r):
                return
            xc, xs = st[("xc", r)]
            bank = ps.tile([P, 512], F32, tag="tin", bufs=4, name="gtbank")
            for jj in range(2):
                j = 2 * b + jj
                for g in range(2):
                    o = N * g + 128 * j
                    nc.tensor.matmul_mx(
                        out=bank[:, 256 * jj : 256 * jj + 256],
                        lhsT=gwc[:, o : o + 128].bitcast(FP8X4),
                        lhsT_scale=gws[:, o : o + 128],
                        rhs=xc[:, 256 * g : 256 * g + 256].bitcast(FP8X4),
                        rhs_scale=xs[:, 256 * g : 256 * g + 256],
                        start=(g == 0),
                        stop=(g == 1),
                    )
            st[("gtbank", r, b)] = bank

        def h_bank(r, b):
            if not okr(r):
                return
            if b == 0:
                st[("gts", r)] = epi_box[0].tile([P, 2048], F32, tag="gts", name="gts", bufs=2)
            gts = st[("gts", r)]
            bank = st[("gtbank", r, b)]
            for jj in range(2):
                j = 2 * b + jj
                nc.scalar.activation(
                    out=gts[:, 256 * j : 256 * j + 256],
                    in_=bank[:, 256 * jj : 256 * jj + 256],
                    func=ACT.Sigmoid,
                    bias=vT[:, j : j + 1],
                )

        def gback(t):
            if not okt(t):
                return
            gts = st[("gts", t // 2)]
            ii = t % 2
            banks = []
            for h in range(2):
                bank = ps.tile([P, 512], F32, tag="gb", name="gbbank")
                for jj in range(4):
                    j = 4 * h + jj
                    nc.tensor.transpose(
                        out=bank[:, 128 * jj : 128 * jj + 128],
                        in_=gts[:, 256 * j + 128 * ii : 256 * j + 128 * ii + 128],
                        identity=idf[:],
                    )
                banks.append(bank)
            st[("gb", t)] = banks

        def syn_mx(t, h):
            if not okt(t):
                return
            zc, zs = st[("zc", t // 2)]
            ii = t % 2
            bank = ps.tile([P, 512], F32, tag="pre", name="prebank")
            for c in range(2):
                o = 256 * c + 128 * ii
                w = N * c + 512 * h
                nc.tensor.matmul_mx(
                    out=bank[:],
                    lhsT=zc[:, o : o + 128].bitcast(FP8X4),
                    lhsT_scale=zs[:, o : o + 128],
                    rhs=sc[:, w : w + 512].bitcast(FP8X4),
                    rhs_scale=ss[:, w : w + 512],
                    start=(c == 0),
                    stop=(c == 1),
                )
            st[("pre", t, h)] = bank

        def op_g(t):
            if not okt(t):
                return
            pt = epi_box[0].tile([P, N], F32, tag="p", name="pt", bufs=3)
            pv = pv_t[t // 2]
            o = N * (t % 2)
            for h in range(2):
                nc.vector.scalar_tensor_tensor(
                    out=pt[:, 512 * h : 512 * h + 512],
                    in0=pv[:, o + 512 * h : o + 512 * h + 512],
                    scalar=DECAY,
                    in1=st[("pre", t, h)][:],
                    op0=ALU.mult,
                    op1=ALU.add,
                )
            nc.sync.dma_start(out=o1_v[:, t, :], in_=pt[:])
            st[("p", t)] = pt

        def op_i(t):
            if not okt(t):
                return
            w = w_box[t % 4]
            pt = st[("p", t)]
            nc.vector.scalar_tensor_tensor(out=w[:, 0:N], in0=pt[:], scalar=SLOPE, in1=pt[:], op0=ALU.mult, op1=ALU.max)
            st[("w", t)] = w

        def op_j(t):
            if not okt(t):
                return
            w = st[("w", t)]
            nc.vector.tensor_tensor(out=w[:, 0:N], in0=w[:, 0:N], in1=x_of(t), op=ALU.subtract)

        def op_k(t):
            if not okt(t):
                return
            w = st[("w", t)]
            se = sml.tile([P, 2], F32, tag="se", name="se")
            for h in range(2):
                nc.vector.scalar_tensor_tensor(
                    out=w[:, 512 * h : 512 * h + 512],
                    in0=w[:, 512 * h : 512 * h + 512],
                    scalar=1.0,
                    in1=st[("gb", t)][h][:],
                    op0=ALU.mult,
                    op1=ALU.mult,
                    accum_out=se[:, h : h + 1],
                )
            st[("se", t)] = se

        def s1(t):
            if not okt(t):
                return
            se = st[("se", t)]
            s1t = sml.tile([P, 1], F32, tag="s1t", name="s1t")
            nc.vector.tensor_tensor(out=s1t[:], in0=se[:, 0:1], in1=se[:, 1:2], op=ALU.add)
            st[("s1t", t)] = s1t

        def s2(t):
            if not okt(t):
                return
            nmc = sml.tile([P, 1], F32, tag="nmc", name="nmc")
            nc.vector.scalar_tensor_tensor(
                out=nmc[:],
                in0=st[("s1t", t)][:],
                scalar=-1.0 / N,
                in1=st[("nm", t // 2)][:, t % 2 : t % 2 + 1],
                op0=ALU.mult,
                op1=ALU.add,
            )
            st[("nmc", t)] = nmc

        def op_l(t):
            if not okt(t):
                return
            w = st[("w", t)]
            nc.vector.scalar_tensor_tensor(
                out=w[:, 0:N], in0=w[:, 0:N], scalar=st[("nmc", t)][:], in1=x_of(t), op0=ALU.add, op1=ALU.add
            )

        def op_m(t):
            if not okt(t):
                return
            if t < 10:
                sq2 = pw_tile(t // 2 + 1)[:, 2 + t % 2 : 3 + t % 2]
            else:
                st[("sq2", t)] = sml.tile([P, 1], F32, tag="sq2", name="sq2")
                sq2 = st[("sq2", t)][:]
            junk = pro.tile([P, N + 2], BF16, tag="junk", name="junk")
            nc.scalar.activation(
                out=junk[:, 0 : N + 1], in_=st[("w", t)][:, 0 : N + 1], func=ACT.Square, scale=1.0 / 32, accum_out=sq2
            )

        def pow_r(t):
            if not okt(t):
                return
            rs2 = sml.tile([P, 1], F32, tag="rs2", name="rs2")
            nc.gpsimd.tensor_tensor(out=rs2[:], in0=st[("sq2", t)][:], in1=mh[:, 0:1], op=ALU.pow)
            st[("rs2", t)] = rs2[:]

        def np_alloc(t):
            if ("o", t) not in st:
                st[("o", t)] = epi_box[0].tile([P, N], F32, tag="o", name="o", bufs=4)
            return st[("o", t)]

        def np_split(t):
            return {14: 384, 15: 0}.get(t, NP_BY_PARITY[t % 2])

        def np_g(t):
            if not okt(t) or t in TAIL_S:
                return
            o = np_alloc(t)
            sp = np_split(t)
            nc.gpsimd.tensor_tensor(out=o[:, 0:sp], in0=st[("w", t)][:, 0:sp], in1=g_b[:, 0:sp], op=ALU.mult)

        def op_np(t):
            if not okt(t) or t in TAIL_S:
                return
            o = np_alloc(t)
            sp = np_split(t)
            nc.vector.tensor_tensor(out=o[:, sp:N], in0=st[("w", t)][:, sp:N], in1=g_b[:, sp:N], op=ALU.mult)

        def tail_a(t):
            if t not in TAIL_S:
                return
            t1 = epi_box[0].tile([P, N], F32, tag="tl", name="t1", bufs=5)
            nc.scalar.activation(out=t1[:], in_=st[("w", t)][:, 0:N], func=ACT.Identity, scale=st[("rs2", t)])
            banks = []
            for h in range(2):
                bank = ps.tile([P, 512], F32, tag="tin", bufs=4, name="tbank")
                for jj in range(4):
                    j = 4 * h + jj
                    nc.tensor.transpose(
                        out=bank[:, 128 * jj : 128 * jj + 128], in_=t1[:, 128 * j : 128 * j + 128], identity=idf[:]
                    )
                banks.append(bank)
            st[("tbank", t)] = banks

        def tail_b(t):
            if t not in TAIL_S:
                return
            oT = epi_box[0].tile([P, N], F32, tag="tl", name="oT", bufs=5)
            for h in range(2):
                for jj in range(4):
                    j = 4 * h + jj
                    nc.scalar.activation(
                        out=oT[:, 128 * j : 128 * j + 128],
                        in_=st[("tbank", t)][h][:, 128 * jj : 128 * jj + 128],
                        func=ACT.Identity,
                        scale=vT[:, 24 + j : 25 + j],
                        bias=vT[:, 32 + j : 33 + j],
                    )
            banks = []
            for h in range(2):
                bank = ps.tile([P, 512], F32, tag="tin", bufs=4, name="ubank")
                for jj in range(4):
                    j = 4 * h + jj
                    nc.tensor.transpose(
                        out=bank[:, 128 * jj : 128 * jj + 128], in_=oT[:, 128 * j : 128 * j + 128], identity=idf[:]
                    )
                banks.append(bank)
            st[("ubank", t)] = banks

        def tail_c(t):
            if t not in TAIL_S:
                return
            of = epi_box[0].tile([P, N], F32, tag="tl", name="of", bufs=5)
            for h in range(2):
                nc.scalar.copy(out=of[:, 512 * h : 512 * h + 512], in_=st[("ubank", t)][h][:])
            nc.sync.dma_start(out=o0_v[:, t, :], in_=of[:])

        def op_o(t, parts=1):
            if not okt(t) or t in TAIL_S:
                return
            o = st[("o", t)]
            for h in range(parts):
                sl = slice(N // parts * h, N // parts * h + N // parts)
                nc.vector.scalar_tensor_tensor(
                    out=o[:, sl], in0=o[:, sl], scalar=st[("rs2", t)], in1=b_b[:, sl], op0=ALU.mult, op1=ALU.add
                )
                nc.sync.dma_start(out=o0_v[:, t, sl], in_=o[:, sl])

        load_x(0)
        load_x(1)
        nc.sync.dma_start(out=vec[0:8, :], in_=gate_b.rearrange("(j m) -> j m", m=P))
        nc.sync.dma_start(out=vec[8:16, :], in_=pre_gamma.rearrange("(j m) -> j m", m=P))
        nc.sync.dma_start(out=vec[16:24, :], in_=pre_beta.rearrange("(j m) -> j m", m=P))
        nc.sync.dma_start(out=vec[24:32, :], in_=ln_gamma.rearrange("(j m) -> j m", m=P))
        nc.sync.dma_start(out=vec[32:40, :], in_=ln_beta.rearrange("(j m) -> j m", m=P))
        with tc.tile_pool(name="wt", bufs=1) as wt:
            sraw = []
            for c in range(2):
                raw = wt.tile([P, 4 * N], BF16, tag="wraw", name="sraw", bufs=4)
                nc.sync.dma_start(out=raw[:].rearrange("p (t n) -> p t n", t=4), in_=syn_v[c])
                sraw.append(raw)
            graw = []
            for h in range(2):
                raw = wt.tile([P, 4 * N], BF16, tag="wraw", name="graw", bufs=4)
                nc.sync.dma_start(out=raw[:].rearrange("p (j k) -> p j k", j=4), in_=gw_v[h])
                graw.append(raw)
            load_pv(0)
            nc.sync.dma_start(out=g_b[:], in_=ln_gamma.partition_broadcast(P))
            nc.sync.dma_start(out=b_b[:], in_=ln_beta.partition_broadcast(P))
            for q in range(2, NQ):
                load_x(q)
                load_pv(q - 1)
            load_pv(NQ - 1)

            def syn_prep(c):
                grps = []
                for h in range(2):
                    grp = wt.tile([P, 2048], BF16, tag="wgrp", name="sgrp", bufs=6, align_bytes=64)
                    nc.vector.tensor_copy(
                        out=grp[:].rearrange("p (a i t) -> p a t i", i=4, t=4),
                        in_=sraw[c][:].rearrange("p (t n) -> p t n", t=4)[:, :, 512 * h : 512 * h + 512].rearrange(
                            "p t (a i) -> p a t i", i=4
                        ),
                    )
                    grps.append(grp)
                for h in range(2):
                    o = N * c + 512 * h
                    nc.vector.quantize_mx(
                        out=sc[:, o : o + 512].bitcast(FP8X4), scales=ss[:, o : o + 512], in_=grps[h][:]
                    )

            def gw_prep(h):
                gww = graw[h][:].bitcast(F32)
                grps = []
                for g in range(2):
                    grp = wt.tile([P, 2048], BF16, tag="wgrp", name="ggrp", bufs=6, align_bytes=64)
                    grw = grp[:].bitcast(F32)
                    for jq in range(2):
                        bank = ps.tile([P, 512], F32, tag="tin", bufs=4, name="gbank")
                        for u in range(2):
                            b = 2 * g + u
                            for j2 in range(2):
                                j = 2 * jq + j2
                                nc.tensor.transpose(
                                    out=bank[:, 256 * u + 128 * j2 : 256 * u + 128 * j2 + 128],
                                    in_=gww[:, 512 * j + 128 * b : 512 * j + 128 * b + 128],
                                    identity=idf[:],
                                )
                        nc.scalar.copy(
                            out=grw[:, 512 * jq : 512 * jq + 512].rearrange("p (n u) -> p n u", u=2),
                            in_=bank[:].rearrange("p (u n) -> p n u", u=2),
                        )
                    grps.append(grp)
                for g in range(2):
                    o = N * g + 512 * h
                    nc.vector.quantize_mx(
                        out=gwc[:, o : o + 512].bitcast(FP8X4), scales=gws[:, o : o + 512], in_=grps[g][:]
                    )

            st6 = sml.tile([P, 24], F32, tag="st6", name="st6", bufs=1)
            mv = sml.tile([P, 4], F32, tag="mv", name="mv", bufs=1)
            for ii in range(2):
                for hh in range(2):
                    k6 = 6 * (2 * ii + hh)
                    nc.vector.bn_stats(
                        out=st6[:, k6 : k6 + 6], in_=x_t[0][:, N * ii + 512 * hh : N * ii + 512 * hh + 512]
                    )
            for ii in range(2):
                nc.vector.bn_aggr(out=mv[:, 2 * ii : 2 * ii + 2], in_=st6[:, 12 * ii : 12 * ii + 12])
            mvv = mv[:].rearrange("p (i s) -> p i s", s=2)
            nm0 = sml.tile([P, 2], F32, tag="nm", name="nm", bufs=6)
            nc.vector.tensor_scalar(out=nm0[:], in0=mvv[:, :, 0], scalar1=-1.0, scalar2=None, op0=ALU.mult)
            va0 = sml.tile([P, 2], F32, tag="va", name="va")
            nc.vector.tensor_scalar(out=va0[:], in0=mvv[:, :, 1], scalar1=EPS, scalar2=None, op0=ALU.add)
            st[("nm", 0)] = nm0
            st[("va", 0)] = va0
            rs0 = sml.tile([P, 4], F32, tag="rs", name="rs")
            nc.gpsimd.tensor_tensor(out=rs0[:, 0:2], in0=va0[:], in1=mh[:, 0:2], op=ALU.pow)
            st[("rs1", 0)] = rs0
            nr0 = sml.tile([P, 2], F32, tag="nr", name="nr")
            nc.vector.tensor_tensor(out=nr0[:], in0=nm0[:], in1=rs0[:, 0:2], op=ALU.mult)
            st[("rs", 0)] = (rs0, nr0)

            xT_pe(0)
            dd(0)
            vbank = ps.tile([P, P], BF16, tag="tin", bufs=4, name="vbank")
            nc.tensor.transpose(out=vbank[:], in_=vec[:], identity=idb[:])
            nc.vector.tensor_copy(out=vT[:, 0:40], in_=vbank[:, 0:40])
            qx(0)
            xT_pe(1)
            dd(1)
            pe_sum(1, 0)
            pe_sum(1, 1)
            cc(0, 0, True)
            cc(0, 1, True)
            syn_prep(0)
            nm_s(1)
            m2_s(1)
            zT_bank(0, 0)
            zT_bank(0, 1)
            e_bank(0, 0)
            zT_bank(0, 2)
            e_bank(0, 1)
            zT_bank(0, 3)
            e_bank(0, 2)
            e_bank(0, 3)
            dg(1)
            va_b(1)
            va_c(1)
            pows(-1)
            qx(1)
            nr_v(1)
            syn_prep(1)
            rg(0, 0, False)
            rg(0, 1, False)
            qz(0)
            gw_prep(0)
            cc(1, 0)
            cc(1, 1)
            gw_prep(1)
            zT_bank(1, 0)
            zT_bank(1, 1)
            e_bank(1, 0)
            zT_bank(1, 2)
            e_bank(1, 1)
            zT_bank(1, 3)
            e_bank(1, 2)
            e_bank(1, 3)
            syn_mx(0, 0)
            syn_mx(0, 1)

        epi_box.append(ctx.enter_context(tc.tile_pool(name="epi", bufs=3)))
        for i in range(4):
            w = epi_box[0].tile([P, N + 8], F32, tag="w%d" % i, name="w", bufs=1)
            nc.gpsimd.memset(w[:, N : N + 1], EPS**0.5 * 32)
            w_box.append(w)

        gate_mx(0, 0)
        gate_mx(0, 1)
        gate_mx(0, 2)
        h_bank(0, 0)
        gate_mx(0, 3)
        h_bank(0, 1)
        h_bank(0, 2)
        h_bank(0, 3)
        op_g(0)
        rg(1, 0, False)
        op_i(0)
        syn_mx(1, 0)
        syn_mx(1, 1)
        gback(0)
        rg(1, 1, False)
        op_j(0)
        xT_pe(2)
        dd(2)

        for tau in range(0, NT - 2):
            m = tau // 2
            if tau % 2 == 0:
                np_g(tau - 1)
                if m > 0:
                    e_bank(m + 1, 2)
                    e_bank(m + 1, 3)
                op_k(tau)
                op_g(tau + 1)
                gback(tau + 1)
                tail_b(tau - 2)
                pe_sum(m + 2, 0)
                pe_sum(m + 2, 1)
                op_m(tau - 1)
                if tau - 1 >= 10:
                    pow_r(tau - 1)
                if m > 0:
                    rg(m + 1, 0, True)
                    rg(m + 1, 1, True)
                nm_s(m + 2)
                op_o(tau - 3)
                s1(tau)
                op_i(tau + 1)
                tail_c(tau - 2)
                gate_mx(m + 1, 0)
                gate_mx(m + 1, 1)
                h_bank(m + 1, 0)
                m2_s(m + 2)
                gate_mx(m + 1, 2)
                h_bank(m + 1, 1)
                gate_mx(m + 1, 3)
                h_bank(m + 1, 2)
                h_bank(m + 1, 3)
                op_np(tau - 1)
                s2(tau)
                op_j(tau + 1)
                dg(m + 2)
                op_l(tau)
                va_b(m + 2)
                qz(m + 1)
                syn_mx(tau + 2, 0)
                syn_mx(tau + 2, 1)
                qx(m + 2)
                va_c(m + 2)
                tail_a(tau - 1)
            else:
                pows(m)
                np_g(tau - 1)
                op_k(tau)
                op_g(tau + 1)
                op_m(tau - 1)
                if tau - 1 >= 10:
                    pow_r(tau - 1)
                syn_mx(tau + 2, 0)
                syn_mx(tau + 2, 1)
                gback(tau + 1)
                nr_s(m + 2)
                cc(m + 2, 0)
                cc(m + 2, 1)
                xT_pe(m + 3)
                dd(m + 3)
                tail_b(tau - 2)
                op_o(tau - 3)
                s1(tau)
                op_i(tau + 1)
                zT_bank(m + 2, 0)
                zT_bank(m + 2, 1)
                op_np(tau - 1)
                s2(tau)
                op_j(tau + 1)
                e_bank(m + 2, 0)
                e_bank(m + 2, 1)
                tail_c(tau - 2)
                zT_bank(m + 2, 2)
                zT_bank(m + 2, 3)
                op_l(tau)
                tail_a(tau - 1)

        op_m(13)
        op_k(14)
        gback(15)
        op_g(15)
        pow_r(13)
        tail_b(12)
        s1(14)
        op_i(15)
        tail_a(13)
        tail_c(12)
        s2(14)
        op_j(15)
        op_l(14)

        np_g(14)
        op_m(14)
        op_k(15)
        pow_r(14)
        tail_b(13)
        s1(15)
        op_np(14)
        s2(15)
        op_l(15)

        op_m(15)
        op_o(14)
        op_np(15)
        pow_r(15)
        tail_c(13)
        op_o(15, 2)
